import numpy as np
import ml_dtypes


def mxq(x, axis, fmt="e4m3"):
    dtype, down = {"e4m3": (ml_dtypes.float8_e4m3fn, 7), "e5m2": (ml_dtypes.float8_e5m2, 14)}[fmt]
    v = np.moveaxis(np.asarray(x, np.float32).astype(ml_dtypes.bfloat16).astype(np.float64), axis, -1)
    blocks = v.reshape(v.shape[:-1] + (-1, 32))
    amax = np.abs(blocks).max(-1, keepdims=True)
    byte = np.maximum(np.where(amax > 0, np.frexp(amax)[1] - 1 + 127, 0) - down, 1)
    scale = np.exp2(byte - 127.0)
    codes = (blocks / scale).astype(np.float32).astype(dtype).astype(np.float64)
    return np.moveaxis((codes * scale).reshape(v.shape), -1, axis)


WIDE = False


def mx_kscale(k):
    if not WIDE:
        return np.ones(k)
    levels = np.array([10, -10, 5, -5, 0])
    a = np.random.permutation(np.resize(levels, k // 512 * 4)).reshape(k // 512, 4)
    idx = np.arange(k)
    return np.exp2(a[idx // 512, idx % 128 // 32])


BF16 = ml_dtypes.bfloat16


def bf(x):
    return np.asarray(x, np.float32).astype(BF16)


def f64(x):
    return np.asarray(x).astype(np.float64)


E, F, H, MID, OUT = 4096, 64, 192, 1024, 256
D = 2 * (F + H)
IN = D + 1


def setup_inputs():
    s = mx_kscale(D)
    t = mx_kscale(MID)
    w1 = np.concatenate([np.random.standard_normal((MID, D)) / np.sqrt(D) / s[None, :],
                         np.random.standard_normal((MID, 1)) * 0.5], axis=1) * t[:, None]
    return {"dst_node_feat": bf(np.random.standard_normal((E, F)) * s[:F]),
            "dst_node_hidden": bf(np.random.standard_normal((E, H)) * s[F:F + H]),
            "src_node_feat": bf(np.random.standard_normal((E, F)) * s[F + H:2 * F + H]),
            "src_node_hidden": bf(np.random.standard_normal((E, H)) * s[2 * F + H:]),
            "edge_feat": bf(np.random.standard_normal(E)),
            "W1": bf(w1),
            "b1": bf(np.random.standard_normal(MID) * 0.3 * t),
            "W2": bf(np.random.standard_normal((OUT, MID)) / np.sqrt(MID) / t[None, :]),
            "b2": bf(np.random.standard_normal(OUT) * 0.3)}


def reference(dst_node_feat, dst_node_hidden, src_node_feat, src_node_hidden, edge_feat, W1, b1, W2, b2):
    x = np.concatenate([f64(dst_node_feat), f64(dst_node_hidden), f64(src_node_feat), f64(src_node_hidden),
                        f64(edge_feat)[:, None]], axis=1)
    w1 = f64(W1)
    pre = (mxq(x[:, :D], 1, "e4m3") @ mxq(w1[:, :D], 1, "e4m3").T) + x[:, D:] * w1[:, D] + f64(b1)
    h = np.maximum(pre, 0.0)
    return np.tanh((mxq(h, 1, "e4m3") @ mxq(f64(W2), 1, "e4m3").T) + f64(b2))

@@ -1,0 +1,289 @@
+from contextlib import ExitStack
+
+import concourse.mybir as mybir
+from concourse.masks import make_identity
+
+F32 = mybir.dt.float32
+BF16 = mybir.dt.bfloat16
+U32 = mybir.dt.uint32
+U8 = mybir.dt.uint8
+FP8X4 = mybir.dt.float8_e4m3fn_x4
+ADD = mybir.AluOpType.add
+MULT = mybir.AluOpType.mult
+RELU = mybir.ActivationFunctionType.Relu
+TANH = mybir.ActivationFunctionType.Tanh
+
+P = 128
+PACK = 4
+EDGES, FEAT, HIDDEN, MID, OUT = 4096, 64, 192, 1024, 256
+NODE = 2 * (FEAT + HIDDEN)
+FLOPS = 2 * EDGES * ((NODE + 1) * MID + MID * OUT)
+
+CHUNK = 512
+BLOCKS = CHUNK // P
+N_CHUNKS = EDGES // CHUNK
+M_TILES = MID // P
+PASSES = M_TILES // PACK
+WORDS = NODE // 2
+W1_PITCH = NODE + 4
+PAIR = 2 * CHUNK
+
+
+def transpose_words(nc, bank, rows, identity):
+    for b in range(2):
+        for u in range(2):
+            nc.tensor.transpose(bank[:, b, u, :], rows[:, b, u * P : (u + 1) * P], identity)
+
+
+def grouped_words(grouped):
+    return grouped.bitcast(F32).rearrange("q (b r u) -> q b r u", r=P, u=2)
+
+
+def tile_edgenetwork_t_kernel(
+    tc,
+    dst_node_feat,
+    dst_node_hidden,
+    src_node_feat,
+    src_node_hidden,
+    edge_feat,
+    W1,
+    b1,
+    W2,
+    b2,
+    out,
+):
+    nc = tc.nc
+    with ExitStack() as ctx:
+        keep = ctx.enter_context(tc.tile_pool(name="keep", bufs=1))
+        x_pool = ctx.enter_context(tc.tile_pool(name="x_rows", bufs=N_CHUNKS))
+        xq_pool = ctx.enter_context(tc.tile_pool(name="x_quantised", bufs=2))
+        term_pool = ctx.enter_context(tc.tile_pool(name="term", bufs=2 * M_TILES))
+        h_pool = ctx.enter_context(tc.tile_pool(name="hidden", bufs=3))
+        hq_pool = ctx.enter_context(tc.tile_pool(name="hidden_quantised", bufs=2))
+        y_pool = ctx.enter_context(tc.tile_pool(name="result", bufs=3))
+        flip_psum = ctx.enter_context(tc.psum_pool(name="flip", bufs=2))
+        h_psum = ctx.enter_context(tc.psum_pool(name="hidden_sums", bufs=4))
+        y_psum = ctx.enter_context(tc.psum_pool(name="result_sums", bufs=2))
+
+        w1_rows = keep.tile([P, M_TILES, W1_PITCH], BF16)
+        w1_dram = W1.rearrange("(j r) k -> r j k", r=P)
+        x_parts = (
+            (dst_node_feat, 0, FEAT),
+            (dst_node_hidden, FEAT, HIDDEN),
+            (src_node_feat, FEAT + HIDDEN, FEAT),
+            (src_node_hidden, 2 * FEAT + HIDDEN, HIDDEN),
+        )
+        x_rows = []
+
+        def load_w1(half):
+            tiles = slice(half * PACK, (half + 1) * PACK)
+            nc.sync.dma_start(out=w1_rows[:, tiles, 0 : NODE + 1], in_=w1_dram[:, tiles, :])
+
+        def load_x(c):
+            rows = x_pool.tile([P, BLOCKS, NODE], BF16, name="x_rows")
+            for part, first, width in x_parts:
+                nc.sync.dma_start(
+                    out=rows[:, :, first : first + width],
+                    in_=part.rearrange("(b r) f -> r b f", r=P)[:, c * BLOCKS : (c + 1) * BLOCKS, :],
+                )
+            x_rows.append(rows)
+
+        edge_all = keep.tile([P, EDGES], BF16)
+
+        def load_edge(pair):
+            cols = slice(pair * PAIR, (pair + 1) * PAIR)
+            nc.sync.dma_start(out=edge_all[:, cols], in_=edge_feat[cols].partition_broadcast(P))
+
+        b1_rows = keep.tile([P, P], BF16)
+        nc.vector.memset(b1_rows[:], 0.0)
+        w2_rows = keep.tile([P, OUT // P, MID], BF16)
+        b2_all = keep.tile([P, OUT], BF16)
+
+        load_w1(0)
+        load_x(0)
+        nc.sync.dma_start(out=b1_rows[0:M_TILES, :], in_=b1.rearrange("(j r) -> j r", r=P))
+        load_w1(1)
+        load_edge(0)
+        load_x(1)
+        nc.sync.dma_start(out=w2_rows[:], in_=W2.rearrange("(a r) m -> r a m", r=P))
+        nc.sync.dma_start(out=b2_all[:], in_=b2.partition_broadcast(P))
+        for c in range(2, N_CHUNKS):
+            if c % 2 == 0:
+                load_edge(c // 2)
+            load_x(c)
+
+        identity_f32 = keep.tile([P, P], F32)
+        make_identity(nc, identity_f32[:])
+        identity_bf16 = keep.tile([P, P], BF16)
+        make_identity(nc, identity_bf16[:])
+
+        w1_words = w1_rows[:].bitcast(F32)
+        w1_grouped = keep.tile([P, MID * PACK], BF16, align_bytes=64)
+        w1_codes = keep.tile([P, MID], U32, align_bytes=64)
+        w1_scales = keep.tile([P, MID], U8, align_bytes=64)
+        for half in range(PASSES):
+            for two in range(half * 2, half * 2 + 2):
+                tiles = slice(2 * two, 2 * two + 2)
+                w1_flip = flip_psum.tile([P, 2, 2, P], F32, tag="flip")
+                transpose_words(nc, w1_flip, w1_words[:, tiles, :], identity_f32[:])
+                nc.vector.tensor_copy(
+                    out=grouped_words(w1_grouped[:])[:, tiles, :, :],
+                    in_=w1_flip[:].rearrange("q b u r -> q b r u"),
+                )
+            units = slice(half * CHUNK, (half + 1) * CHUNK)
+            nc.vector.quantize_mx(
+                out=w1_codes[:, units].bitcast(FP8X4),
+                scales=w1_scales[:, units],
+                in_=w1_grouped[:, half * CHUNK * PACK : (half + 1) * CHUNK * PACK],
+            )
+
+        w1_edge = keep.tile([P, M_TILES], F32)
+        nc.vector.tensor_copy(out=w1_edge[:], in_=w1_rows[:, :, NODE])
+        b1_flip = flip_psum.tile([P, P], BF16, tag="flip")
+        nc.tensor.transpose(b1_flip[:], b1_rows[:], identity_bf16[:])
+        b1_cols = keep.tile([P, M_TILES], F32)
+        nc.vector.tensor_copy(out=b1_cols[:], in_=b1_flip[:, 0:M_TILES])
+
+        x_codes = {}
+        x_scales = {}
+
+        def quantise_x(c):
+            words = x_rows[c][:].bitcast(F32)
+            grouped = xq_pool.tile([P, CHUNK * PACK], BF16, align_bytes=64, name="x_grouped")
+            for two in range(BLOCKS // 2):
+                blocks = slice(2 * two, 2 * two + 2)
+                x_flip = flip_psum.tile([P, 2, 2, P], F32, tag="flip")
+                transpose_words(nc, x_flip, words[:, blocks, :], identity_f32[:])
+                nc.scalar.copy(
+                    out=grouped_words(grouped[:])[:, blocks, :, :],
+                    in_=x_flip[:].rearrange("q b u r -> q b r u"),
+                )
+            x_codes[c] = xq_pool.tile([P, CHUNK], U32, align_bytes=64, name="x_codes")
+            x_scales[c] = xq_pool.tile([P, CHUNK], U8, align_bytes=64, name="x_scales")
+            nc.vector.quantize_mx(
+                out=x_codes[c][:].bitcast(FP8X4), scales=x_scales[c][:], in_=grouped[:]
+            )
+
+        terms = {}
+
+        def unquantised_term(pair):
+            for j in range(M_TILES):
+                terms[pair, j] = term_pool.tile([P, PAIR], F32, name="term")
+                nc.gpsimd.tensor_scalar(
+                    out=terms[pair, j][:],
+                    in0=edge_all[:, pair * PAIR : (pair + 1) * PAIR],
+                    scalar1=w1_edge[:, j : j + 1],
+                    scalar2=b1_cols[:, j : j + 1],
+                    op0=MULT,
+                    op1=ADD,
+                )
+
+        pre = {}
+        h_grouped = {}
+        h_codes = {}
+        h_scales = {}
+
+        def project(c, g):
+            pre[c, g] = h_pool.tile([P, PACK, CHUNK], BF16, name="pre")
+            for t in range(PACK):
+                j = g * PACK + t
+                sums = h_psum.tile([P, CHUNK], F32, name="sums")
+                nc.tensor.matmul_mx(
+                    out=sums[:],
+                    lhsT=w1_codes[:, j * P : (j + 1) * P].bitcast(FP8X4),
+                    lhsT_scale=w1_scales[:, j * P : (j + 1) * P],
+                    rhs=x_codes[c][:].bitcast(FP8X4),
+                    rhs_scale=x_scales[c][:],
+                    start=True,
+                    stop=True,
+                )
+                first = (c % 2) * CHUNK
+                nc.vector.tensor_tensor(
+                    out=pre[c, g][:, t, :],
+                    in0=sums[:],
+                    in1=terms[c // 2, j][:, first : first + CHUNK],
+                    op=ADD,
+                )
+
+        def rectify(c, g):
+            h_grouped[c, g] = h_pool.tile([P, CHUNK, PACK], BF16, align_bytes=64, name="h_grouped")
+            nc.scalar.activation(
+                out=h_grouped[c, g][:], in_=pre[c, g][:].rearrange("r t e -> r e t"), func=RELU
+            )
+
+        def quantise_h(c, g):
+            if g == 0:
+                h_codes[c] = hq_pool.tile([P, PASSES, CHUNK], U32, align_bytes=64, name="h_codes")
+                h_scales[c] = hq_pool.tile([P, PASSES, CHUNK], U8, align_bytes=64, name="h_scales")
+            nc.vector.quantize_mx(
+                out=h_codes[c][:, g, :].bitcast(FP8X4),
+                scales=h_scales[c][:, g, :],
+                in_=h_grouped[c, g][:].rearrange("r e t -> r (e t)"),
+            )
+
+        out_dram = out.rearrange("(b r) o -> r b o", r=P)
+
+        def finish(c):
+            y = y_pool.tile([P, BLOCKS, OUT], F32, name="y")
+            for two in range(BLOCKS // 2):
+                y_sums = y_psum.tile([P, 2, OUT], F32, name="y_sums")
+                for i in range(2):
+                    edges = slice((2 * two + i) * P, (2 * two + i + 1) * P)
+                    for g in range(PASSES):
+                        nc.tensor.matmul_mx(
+                            out=y_sums[:, i, :],
+                            lhsT=h_codes[c][:, g, edges].bitcast(FP8X4),
+                            lhsT_scale=h_scales[c][:, g, edges],
+                            rhs=w2_codes[:, g, :].bitcast(FP8X4),
+                            rhs_scale=w2_scales[:, g, :],
+                            start=(g == 0),
+                            stop=(g == PASSES - 1),
+                        )
+                nc.vector.tensor_tensor(
+                    out=y[:, 2 * two : 2 * two + 2, :],
+                    in0=y_sums[:],
+                    in1=b2_all[:].unsqueeze(1).to_broadcast([P, 2, OUT]),
+                    op=ADD,
+                )
+            nc.scalar.activation(out=y[:], in_=y[:], func=TANH)
+            nc.sync.dma_start(out=out_dram[:, c * BLOCKS : (c + 1) * BLOCKS, :], in_=y[:])
+
+        quantise_x(0)
+        unquantised_term(0)
+
+        w2_grouped = keep.tile([P, PASSES, OUT, PACK], BF16, align_bytes=64)
+        w2_codes = keep.tile([P, PASSES, OUT], U32, align_bytes=64)
+        w2_scales = keep.tile([P, PASSES, OUT], U8, align_bytes=64)
+        for g in range(PASSES):
+            w2_flip = flip_psum.tile([P, PACK, OUT], BF16, tag="flip")
+            for t in range(PACK):
+                for a in range(OUT // P):
+                    first = (g * PACK + t) * P
+                    nc.tensor.transpose(
+                        w2_flip[:, t, a * P : (a + 1) * P],
+                        w2_rows[:, a, first : first + P],
+                        identity_bf16[:],
+                    )
+            nc.vector.tensor_copy(
+                out=w2_grouped[:, g, :, :], in_=w2_flip[:].rearrange("r t o -> r o t")
+            )
+        nc.vector.quantize_mx(
+            out=w2_codes[:].rearrange("r g o -> r (g o)").bitcast(FP8X4),
+            scales=w2_scales[:].rearrange("r g o -> r (g o)"),
+            in_=w2_grouped[:].rearrange("r g o t -> r (g o t)"),
+        )
+
+        steps = [(c, g) for c in range(N_CHUNKS) for g in range(PASSES)]
+        for n, (c, g) in enumerate(steps):
+            if g == 0 and c + 1 < N_CHUNKS:
+                quantise_x(c + 1)
+            if g == 0 and c % 2 == 0 and c // 2 + 1 < N_CHUNKS // 2:
+                unquantised_term(c // 2 + 1)
+            project(c, g)
+            rectify(c, g)
+            if n >= 1:
+                quantise_h(*steps[n - 1])
+            if g == 1 and c >= 1:
+                finish(c - 1)
+        quantise_h(*steps[-1])
+        finish(N_CHUNKS - 1)

@@ -25,7 +25,7 @@ N_CHUNKS = EDGES // CHUNK
 M_TILES = MID // P
 PASSES = M_TILES // PACK
 WORDS = NODE // 2
-W1_PITCH = NODE + 4
+W1_PITCH = NODE + 16
 PAIR = 2 * CHUNK
 
 
@@ -60,10 +60,11 @@ def tile_edgenetwork_t_kernel(
         term_pool = ctx.enter_context(tc.tile_pool(name="term", bufs=2 * M_TILES))
         h_pool = ctx.enter_context(tc.tile_pool(name="hidden", bufs=3))
         hq_pool = ctx.enter_context(tc.tile_pool(name="hidden_quantised", bufs=2))
-        y_pool = ctx.enter_context(tc.tile_pool(name="result", bufs=3))
+        y_pool = ctx.enter_context(tc.tile_pool(name="result", bufs=4))
         flip_psum = ctx.enter_context(tc.psum_pool(name="flip", bufs=2))
         h_psum = ctx.enter_context(tc.psum_pool(name="hidden_sums", bufs=4))
         y_psum = ctx.enter_context(tc.psum_pool(name="result_sums", bufs=2))
+        ctx.enter_context(tc.manual_schedule())
 
         w1_rows = keep.tile([P, M_TILES, W1_PITCH], BF16)
         w1_dram = W1.rearrange("(j r) k -> r j k", r=P)
@@ -75,8 +76,8 @@ def tile_edgenetwork_t_kernel(
         )
         x_rows = []
 
-        def load_w1(half):
-            tiles = slice(half * PACK, (half + 1) * PACK)
+        def load_w1(two):
+            tiles = slice(2 * two, 2 * two + 2)
             nc.sync.dma_start(out=w1_rows[:, tiles, 0 : NODE + 1], in_=w1_dram[:, tiles, :])
 
         def load_x(c):
@@ -99,11 +100,13 @@ def tile_edgenetwork_t_kernel(
         w2_rows = keep.tile([P, OUT // P, MID], BF16)
         b2_all = keep.tile([P, OUT], BF16)
 
-        load_w1(0)
-        load_x(0)
         nc.sync.dma_start(out=b1_rows[0:M_TILES, :], in_=b1.rearrange("(j r) -> j r", r=P))
-        load_w1(1)
         load_edge(0)
+        load_w1(0)
+        load_w1(1)
+        load_x(0)
+        load_w1(2)
+        load_w1(3)
         load_x(1)
         nc.sync.dma_start(out=w2_rows[:], in_=W2.rearrange("(a r) m -> r a m", r=P))
         nc.sync.dma_start(out=b2_all[:], in_=b2.partition_broadcast(P))
@@ -112,56 +115,32 @@ def tile_edgenetwork_t_kernel(
                 load_edge(c // 2)
             load_x(c)
 
-        identity_f32 = keep.tile([P, P], F32)
-        make_identity(nc, identity_f32[:])
         identity_bf16 = keep.tile([P, P], BF16)
         make_identity(nc, identity_bf16[:])
+        identity_f32 = keep.tile([P, P], F32)
+        make_identity(nc, identity_f32[:])
 
-        w1_words = w1_rows[:].bitcast(F32)
-        w1_grouped = keep.tile([P, MID * PACK], BF16, align_bytes=64)
-        w1_codes = keep.tile([P, MID], U32, align_bytes=64)
-        w1_scales = keep.tile([P, MID], U8, align_bytes=64)
-        for half in range(PASSES):
-            for two in range(half * 2, half * 2 + 2):
-                tiles = slice(2 * two, 2 * two + 2)
-                w1_flip = flip_psum.tile([P, 2, 2, P], F32, tag="flip")
-                transpose_words(nc, w1_flip, w1_words[:, tiles, :], identity_f32[:])
-                nc.vector.tensor_copy(
-                    out=grouped_words(w1_grouped[:])[:, tiles, :, :],
-                    in_=w1_flip[:].rearrange("q b u r -> q b r u"),
-                )
-            units = slice(half * CHUNK, (half + 1) * CHUNK)
-            nc.vector.quantize_mx(
-                out=w1_codes[:, units].bitcast(FP8X4),
-                scales=w1_scales[:, units],
-                in_=w1_grouped[:, half * CHUNK * PACK : (half + 1) * CHUNK * PACK],
-            )
-
-        w1_edge = keep.tile([P, M_TILES], F32)
-        nc.vector.tensor_copy(out=w1_edge[:], in_=w1_rows[:, :, NODE])
-        b1_flip = flip_psum.tile([P, P], BF16, tag="flip")
-        nc.tensor.transpose(b1_flip[:], b1_rows[:], identity_bf16[:])
-        b1_cols = keep.tile([P, M_TILES], F32)
-        nc.vector.tensor_copy(out=b1_cols[:], in_=b1_flip[:, 0:M_TILES])
-
+        x_grouped = {}
         x_codes = {}
         x_scales = {}
 
-        def quantise_x(c):
+        def flip_x(c):
             words = x_rows[c][:].bitcast(F32)
-            grouped = xq_pool.tile([P, CHUNK * PACK], BF16, align_bytes=64, name="x_grouped")
+            x_grouped[c] = xq_pool.tile([P, CHUNK * PACK], BF16, align_bytes=64, name="x_grouped")
             for two in range(BLOCKS // 2):
                 blocks = slice(2 * two, 2 * two + 2)
                 x_flip = flip_psum.tile([P, 2, 2, P], F32, tag="flip")
                 transpose_words(nc, x_flip, words[:, blocks, :], identity_f32[:])
                 nc.scalar.copy(
-                    out=grouped_words(grouped[:])[:, blocks, :, :],
+                    out=grouped_words(x_grouped[c][:])[:, blocks, :, :],
                     in_=x_flip[:].rearrange("q b u r -> q b r u"),
                 )
+
+        def quantise_x(c):
             x_codes[c] = xq_pool.tile([P, CHUNK], U32, align_bytes=64, name="x_codes")
             x_scales[c] = xq_pool.tile([P, CHUNK], U8, align_bytes=64, name="x_scales")
             nc.vector.quantize_mx(
-                out=x_codes[c][:].bitcast(FP8X4), scales=x_scales[c][:], in_=grouped[:]
+                out=x_codes[c][:].bitcast(FP8X4), scales=x_scales[c][:], in_=x_grouped[c][:]
             )
 
         terms = {}
@@ -187,7 +166,7 @@ def tile_edgenetwork_t_kernel(
             pre[c, g] = h_pool.tile([P, PACK, CHUNK], BF16, name="pre")
             for t in range(PACK):
                 j = g * PACK + t
-                sums = h_psum.tile([P, CHUNK], F32, name="sums")
+                sums = h_psum.tile([P, CHUNK], F32, tag="sums")
                 nc.tensor.matmul_mx(
                     out=sums[:],
                     lhsT=w1_codes[:, j * P : (j + 1) * P].bitcast(FP8X4),
@@ -224,9 +203,8 @@ def tile_edgenetwork_t_kernel(
         out_dram = out.rearrange("(b r) o -> r b o", r=P)
 
         def finish(c):
-            y = y_pool.tile([P, BLOCKS, OUT], F32, name="y")
             for two in range(BLOCKS // 2):
-                y_sums = y_psum.tile([P, 2, OUT], F32, name="y_sums")
+                y_sums = y_psum.tile([P, 2, OUT], F32, tag="y_sums")
                 for i in range(2):
                     edges = slice((2 * two + i) * P, (2 * two + i + 1) * P)
                     for g in range(PASSES):
@@ -239,51 +217,99 @@ def tile_edgenetwork_t_kernel(
                             start=(g == 0),
                             stop=(g == PASSES - 1),
                         )
+                y = y_pool.tile([P, 2, OUT], F32, name="y")
                 nc.vector.tensor_tensor(
-                    out=y[:, 2 * two : 2 * two + 2, :],
+                    out=y[:],
                     in0=y_sums[:],
                     in1=b2_all[:].unsqueeze(1).to_broadcast([P, 2, OUT]),
                     op=ADD,
                 )
-            nc.scalar.activation(out=y[:], in_=y[:], func=TANH)
-            nc.sync.dma_start(out=out_dram[:, c * BLOCKS : (c + 1) * BLOCKS, :], in_=y[:])
+                nc.scalar.activation(out=y[:], in_=y[:], func=TANH)
+                first = c * BLOCKS + 2 * two
+                nc.sync.dma_start(out=out_dram[:, first : first + 2, :], in_=y[:])
 
+        b1_flip = y_psum.tile([P, P], BF16, tag="y_sums")
+        nc.tensor.transpose(b1_flip[:], b1_rows[:], identity_bf16[:])
+        b1_cols = keep.tile([P, M_TILES], F32)
+        nc.vector.tensor_copy(out=b1_cols[:], in_=b1_flip[:, 0:M_TILES])
+
+        w1_words = w1_rows[:].bitcast(F32)
+        w1_edge = keep.tile([P, M_TILES], F32)
+        w1_grouped = keep.tile([P, MID * PACK], BF16, align_bytes=64)
+        w1_codes = keep.tile([P, MID], U32, align_bytes=64)
+        w1_scales = keep.tile([P, MID], U8, align_bytes=64)
+
+        def quantise_w1(two):
+            units = slice(two * 2 * P, (two + 1) * 2 * P)
+            nc.vector.quantize_mx(
+                out=w1_codes[:, units].bitcast(FP8X4),
+                scales=w1_scales[:, units],
+                in_=w1_grouped[:, two * 2 * P * PACK : (two + 1) * 2 * P * PACK],
+            )
+
+        def flip_w1(two):
+            tiles = slice(2 * two, 2 * two + 2)
+            nc.vector.tensor_copy(out=w1_edge[:, tiles], in_=w1_rows[:, tiles, NODE])
+            w1_flip = h_psum.tile([P, 2, 2, P], F32, tag="sums")
+            transpose_words(nc, w1_flip, w1_words[:, tiles, :], identity_f32[:])
+            nc.vector.tensor_copy(
+                out=grouped_words(w1_grouped[:])[:, tiles, :, :],
+                in_=w1_flip[:].rearrange("q b u r -> q b r u"),
+            )
+
+        flip_w1(0)
+        flip_w1(1)
+        quantise_w1(0)
+        flip_x(0)
+        quantise_w1(1)
         quantise_x(0)
+        flip_w1(2)
+        flip_w1(3)
+        quantise_w1(2)
+        quantise_w1(3)
         unquantised_term(0)
 
         w2_grouped = keep.tile([P, PASSES, OUT, PACK], BF16, align_bytes=64)
         w2_codes = keep.tile([P, PASSES, OUT], U32, align_bytes=64)
         w2_scales = keep.tile([P, PASSES, OUT], U8, align_bytes=64)
-        for g in range(PASSES):
-            w2_flip = flip_psum.tile([P, PACK, OUT], BF16, tag="flip")
-            for t in range(PACK):
-                for a in range(OUT // P):
-                    first = (g * PACK + t) * P
-                    nc.tensor.transpose(
-                        w2_flip[:, t, a * P : (a + 1) * P],
-                        w2_rows[:, a, first : first + P],
-                        identity_bf16[:],
-                    )
-            nc.vector.tensor_copy(
-                out=w2_grouped[:, g, :, :], in_=w2_flip[:].rearrange("r t o -> r o t")
-            )
-        nc.vector.quantize_mx(
-            out=w2_codes[:].rearrange("r g o -> r (g o)").bitcast(FP8X4),
-            scales=w2_scales[:].rearrange("r g o -> r (g o)"),
-            in_=w2_grouped[:].rearrange("r g o t -> r (g o t)"),
-        )
 
-        steps = [(c, g) for c in range(N_CHUNKS) for g in range(PASSES)]
-        for n, (c, g) in enumerate(steps):
-            if g == 0 and c + 1 < N_CHUNKS:
-                quantise_x(c + 1)
-            if g == 0 and c % 2 == 0 and c // 2 + 1 < N_CHUNKS // 2:
+        def quantise_w2():
+            for g in range(PASSES):
+                w2_flip = y_psum.tile([P, PACK, OUT], BF16, tag="y_sums")
+                for t in range(PACK):
+                    for a in range(OUT // P):
+                        first = (g * PACK + t) * P
+                        nc.tensor.transpose(
+                            w2_flip[:, t, a * P : (a + 1) * P],
+                            w2_rows[:, a, first : first + P],
+                            identity_bf16[:],
+                        )
+                nc.scalar.copy(
+                    out=w2_grouped[:, g, :, :], in_=w2_flip[:].rearrange("r t o -> r o t")
+                )
+            nc.vector.quantize_mx(
+                out=w2_codes[:].rearrange("r g o -> r (g o)").bitcast(FP8X4),
+                scales=w2_scales[:].rearrange("r g o -> r (g o)"),
+                in_=w2_grouped[:].rearrange("r g o t -> r (g o t)"),
+            )
+
+        for c in range(N_CHUNKS):
+            project(c, 0)
+            if c + 1 < N_CHUNKS:
+                flip_x(c + 1)
+            if c % 2 == 0 and c // 2 + 1 < N_CHUNKS // 2:
                 unquantised_term(c // 2 + 1)
-            project(c, g)
-            rectify(c, g)
-            if n >= 1:
-                quantise_h(*steps[n - 1])
-            if g == 1 and c >= 1:
+            if c >= 1:
+                quantise_h(c - 1, 1)
+            if c + 1 < N_CHUNKS:
+                quantise_x(c + 1)
+            rectify(c, 0)
+            project(c, 1)
+            if c == 0:
+                quantise_w2()
+            quantise_h(c, 0)
+            rectify(c, 1)
+            if c >= 1:
                 finish(c - 1)
-        quantise_h(*steps[-1])
+        quantise_h(N_CHUNKS - 1, 1)
         finish(N_CHUNKS - 1)

@@ -24,6 +24,7 @@ BLOCKS = CHUNK // P
 N_CHUNKS = EDGES // CHUNK
 M_TILES = MID // P
 PASSES = M_TILES // PACK
+O_TILES = OUT // P
 WORDS = NODE // 2
 W1_PITCH = NODE + 16
 PAIR = 2 * CHUNK
@@ -60,6 +61,7 @@ def tile_edgenetwork_t_kernel(
         term_pool = ctx.enter_context(tc.tile_pool(name="term", bufs=2 * M_TILES))
         h_pool = ctx.enter_context(tc.tile_pool(name="hidden", bufs=3))
         hq_pool = ctx.enter_context(tc.tile_pool(name="hidden_quantised", bufs=2))
+        yt_pool = ctx.enter_context(tc.tile_pool(name="result_flipped", bufs=3))
         y_pool = ctx.enter_context(tc.tile_pool(name="result", bufs=4))
         flip_psum = ctx.enter_context(tc.psum_pool(name="flip", bufs=2))
         h_psum = ctx.enter_context(tc.psum_pool(name="hidden_sums", bufs=4))
@@ -95,12 +97,14 @@ def tile_edgenetwork_t_kernel(
             cols = slice(pair * PAIR, (pair + 1) * PAIR)
             nc.sync.dma_start(out=edge_all[:, cols], in_=edge_feat[cols].partition_broadcast(P))
 
-        b1_rows = keep.tile([P, P], BF16)
-        nc.vector.memset(b1_rows[:], 0.0)
-        w2_rows = keep.tile([P, OUT // P, MID], BF16)
-        b2_all = keep.tile([P, OUT], BF16)
+        bias_rows = keep.tile([P, P], BF16)
+        nc.vector.memset(bias_rows[:], 0.0)
+        w2_rows = keep.tile([P, O_TILES, MID], BF16)
 
-        nc.sync.dma_start(out=b1_rows[0:M_TILES, :], in_=b1.rearrange("(j r) -> j r", r=P))
+        nc.sync.dma_start(out=bias_rows[0:M_TILES, :], in_=b1.rearrange("(j r) -> j r", r=P))
+        nc.sync.dma_start(
+            out=bias_rows[M_TILES : M_TILES + O_TILES, :], in_=b2.rearrange("(a r) -> a r", r=P)
+        )
         load_edge(0)
         load_w1(0)
         load_w1(1)
@@ -109,7 +113,6 @@ def tile_edgenetwork_t_kernel(
         load_w1(3)
         load_x(1)
         nc.sync.dma_start(out=w2_rows[:], in_=W2.rearrange("(a r) m -> r a m", r=P))
-        nc.sync.dma_start(out=b2_all[:], in_=b2.partition_broadcast(P))
         for c in range(2, N_CHUNKS):
             if c % 2 == 0:
                 load_edge(c // 2)
@@ -152,7 +155,7 @@ def tile_edgenetwork_t_kernel(
                     out=terms[pair, j][:],
                     in0=edge_all[:, pair * PAIR : (pair + 1) * PAIR],
                     scalar1=w1_edge[:, j : j + 1],
-                    scalar2=b1_cols[:, j : j + 1],
+                    scalar2=bias_cols[:, j : j + 1],
                     op0=MULT,
                     op1=ADD,
                 )
@@ -187,7 +190,9 @@ def tile_edgenetwork_t_kernel(
         def rectify(c, g):
             h_grouped[c, g] = h_pool.tile([P, CHUNK, PACK], BF16, align_bytes=64, name="h_grouped")
             nc.scalar.activation(
-                out=h_grouped[c, g][:], in_=pre[c, g][:].rearrange("r t e -> r e t"), func=RELU
+                out=h_grouped[c, g][:].rearrange("r (n i) t -> r n t i", i=PACK),
+                in_=pre[c, g][:].rearrange("r t (n i) -> r n t i", i=PACK),
+                func=RELU,
             )
 
         def quantise_h(c, g):
@@ -202,36 +207,47 @@ def tile_edgenetwork_t_kernel(
 
         out_dram = out.rearrange("(b r) o -> r b o", r=P)
 
-        def finish(c):
+        y_flipped = {}
+
+        def second_matmul(c):
+            y_flipped[c] = yt_pool.tile([P, O_TILES, CHUNK], F32, name="y_flipped")
+            for a in range(O_TILES):
+                y_sums = y_psum.tile([P, CHUNK], F32, tag="y_sums")
+                for g in range(PASSES):
+                    nc.tensor.matmul_mx(
+                        out=y_sums[:],
+                        lhsT=w2_codes[:, g, a * P : (a + 1) * P].bitcast(FP8X4),
+                        lhsT_scale=w2_scales[:, g, a * P : (a + 1) * P],
+                        rhs=h_codes[c][:, g, :].bitcast(FP8X4),
+                        rhs_scale=h_scales[c][:, g, :],
+                        start=(g == 0),
+                        stop=(g == PASSES - 1),
+                    )
+                nc.scalar.activation(
+                    out=y_flipped[c][:, a, :],
+                    in_=y_sums[:],
+                    func=TANH,
+                    bias=bias_cols[:, M_TILES + a : M_TILES + a + 1],
+                )
+
+        def store_result(c):
             for two in range(BLOCKS // 2):
-                y_sums = y_psum.tile([P, 2, OUT], F32, tag="y_sums")
+                y_flip = flip_psum.tile([P, 2, OUT], F32, tag="flip")
                 for i in range(2):
                     edges = slice((2 * two + i) * P, (2 * two + i + 1) * P)
-                    for g in range(PASSES):
-                        nc.tensor.matmul_mx(
-                            out=y_sums[:, i, :],
-                            lhsT=h_codes[c][:, g, edges].bitcast(FP8X4),
-                            lhsT_scale=h_scales[c][:, g, edges],
-                            rhs=w2_codes[:, g, :].bitcast(FP8X4),
-                            rhs_scale=w2_scales[:, g, :],
-                            start=(g == 0),
-                            stop=(g == PASSES - 1),
+                    for a in range(O_TILES):
+                        nc.tensor.transpose(
+                            y_flip[:, i, a * P : (a + 1) * P], y_flipped[c][:, a, edges], identity_f32[:]
                         )
                 y = y_pool.tile([P, 2, OUT], F32, name="y")
-                nc.vector.tensor_tensor(
-                    out=y[:],
-                    in0=y_sums[:],
-                    in1=b2_all[:].unsqueeze(1).to_broadcast([P, 2, OUT]),
-                    op=ADD,
-                )
-                nc.scalar.activation(out=y[:], in_=y[:], func=TANH)
+                nc.scalar.copy(out=y[:], in_=y_flip[:])
                 first = c * BLOCKS + 2 * two
                 nc.sync.dma_start(out=out_dram[:, first : first + 2, :], in_=y[:])
 
-        b1_flip = y_psum.tile([P, P], BF16, tag="y_sums")
-        nc.tensor.transpose(b1_flip[:], b1_rows[:], identity_bf16[:])
-        b1_cols = keep.tile([P, M_TILES], F32)
-        nc.vector.tensor_copy(out=b1_cols[:], in_=b1_flip[:, 0:M_TILES])
+        bias_flip = y_psum.tile([P, P], BF16, tag="y_sums")
+        nc.tensor.transpose(bias_flip[:], bias_rows[:], identity_bf16[:])
+        bias_cols = keep.tile([P, M_TILES + O_TILES], F32)
+        nc.vector.tensor_copy(out=bias_cols[:], in_=bias_flip[:, 0 : M_TILES + O_TILES])
 
         w1_words = w1_rows[:].bitcast(F32)
         w1_edge = keep.tile([P, M_TILES], F32)
@@ -277,7 +293,7 @@ def tile_edgenetwork_t_kernel(
             for g in range(PASSES):
                 w2_flip = y_psum.tile([P, PACK, OUT], BF16, tag="y_sums")
                 for t in range(PACK):
-                    for a in range(OUT // P):
+                    for a in range(O_TILES):
                         first = (g * PACK + t) * P
                         nc.tensor.transpose(
                             w2_flip[:, t, a * P : (a + 1) * P],
@@ -293,23 +309,27 @@ def tile_edgenetwork_t_kernel(
                 in_=w2_grouped[:].rearrange("r g o t -> r (g o t)"),
             )
 
-        for c in range(N_CHUNKS):
-            project(c, 0)
+        for c in range(N_CHUNKS + 2):
+            if c < N_CHUNKS:
+                project(c, 0)
             if c + 1 < N_CHUNKS:
                 flip_x(c + 1)
             if c % 2 == 0 and c // 2 + 1 < N_CHUNKS // 2:
                 unquantised_term(c // 2 + 1)
-            if c >= 1:
+            if 1 <= c <= N_CHUNKS:
                 quantise_h(c - 1, 1)
             if c + 1 < N_CHUNKS:
                 quantise_x(c + 1)
-            rectify(c, 0)
-            project(c, 1)
+            if c < N_CHUNKS:
+                rectify(c, 0)
+                project(c, 1)
             if c == 0:
                 quantise_w2()
-            quantise_h(c, 0)
-            rectify(c, 1)
-            if c >= 1:
-                finish(c - 1)
-        quantise_h(N_CHUNKS - 1, 1)
-        finish(N_CHUNKS - 1)
+            if 1 <= c <= N_CHUNKS:
+                second_matmul(c - 1)
+            if c < N_CHUNKS:
+                quantise_h(c, 0)
+            if c >= 2:
+                store_result(c - 2)
+            if c < N_CHUNKS:
+                rectify(c, 1)

@@ -25,9 +25,7 @@ N_CHUNKS = EDGES // CHUNK
 M_TILES = MID // P
 PASSES = M_TILES // PACK
 O_TILES = OUT // P
-WORDS = NODE // 2
 W1_PITCH = NODE + 16
-PAIR = 2 * CHUNK
 
 
 def transpose_words(nc, bank, rows, identity):
@@ -68,6 +66,10 @@ def tile_edgenetwork_t_kernel(
         y_psum = ctx.enter_context(tc.psum_pool(name="result_sums", bufs=2))
         ctx.enter_context(tc.manual_schedule())
 
+        warm = keep.tile([P, 1], F32)
+        nc.vector.memset(warm[:], 0.0)
+        nc.scalar.activation(out=warm[:], in_=warm[:], func=TANH)
+
         w1_rows = keep.tile([P, M_TILES, W1_PITCH], BF16)
         w1_dram = W1.rearrange("(j r) k -> r j k", r=P)
         x_parts = (
@@ -93,8 +95,8 @@ def tile_edgenetwork_t_kernel(
 
         edge_all = keep.tile([P, EDGES], BF16)
 
-        def load_edge(pair):
-            cols = slice(pair * PAIR, (pair + 1) * PAIR)
+        def load_edge(c, n_chunks):
+            cols = slice(c * CHUNK, (c + n_chunks) * CHUNK)
             nc.sync.dma_start(out=edge_all[:, cols], in_=edge_feat[cols].partition_broadcast(P))
 
         bias_rows = keep.tile([P, P], BF16)
@@ -105,23 +107,77 @@ def tile_edgenetwork_t_kernel(
         nc.sync.dma_start(
             out=bias_rows[M_TILES : M_TILES + O_TILES, :], in_=b2.rearrange("(a r) -> a r", r=P)
         )
-        load_edge(0)
-        load_w1(0)
-        load_w1(1)
         load_x(0)
+        load_w1(0)
+        load_edge(0, 1)
+        load_w1(1)
+        load_edge(1, 1)
         load_w1(2)
         load_w1(3)
         load_x(1)
         nc.sync.dma_start(out=w2_rows[:], in_=W2.rearrange("(a r) m -> r a m", r=P))
         for c in range(2, N_CHUNKS):
             if c % 2 == 0:
-                load_edge(c // 2)
+                load_edge(c, 2)
             load_x(c)
 
         identity_bf16 = keep.tile([P, P], BF16)
         make_identity(nc, identity_bf16[:])
         identity_f32 = keep.tile([P, P], F32)
         make_identity(nc, identity_f32[:])
+
+        bias_flip = y_psum.tile([P, P], BF16, tag="y_sums")
+        nc.tensor.transpose(bias_flip[:], bias_rows[:], identity_bf16[:])
+        bias_cols = keep.tile([P, M_TILES + O_TILES], F32)
+        nc.vector.tensor_copy(out=bias_cols[:], in_=bias_flip[:, 0 : M_TILES + O_TILES])
+
+        w1_words = w1_rows[:].bitcast(F32)
+        w1_edge = [keep.tile([P, PACK], F32, name="w1_edge_%d" % g) for g in range(PASSES)]
+        w1_grouped = keep.tile([P, MID * PACK], BF16, align_bytes=64)
+        w1_codes = keep.tile([P, MID], U32, align_bytes=64)
+        w1_scales = keep.tile([P, MID], U8, align_bytes=64)
+
+        def flip_w1(two, bank, copy):
+            tiles = slice(2 * two, 2 * two + 2)
+            first = (2 * two) % PACK
+            copy(out=w1_edge[2 * two // PACK][:, first : first + 2], in_=w1_rows[:, tiles, NODE])
+            transpose_words(nc, bank, w1_words[:, tiles, :], identity_f32[:])
+            copy(
+                out=grouped_words(w1_grouped[:])[:, tiles, :, :],
+                in_=bank[:].rearrange("q b u r -> q b r u"),
+            )
+
+        def quantise_w1(two):
+            units = slice(two * 2 * P, (two + 1) * 2 * P)
+            nc.vector.quantize_mx(
+                out=w1_codes[:, units].bitcast(FP8X4),
+                scales=w1_scales[:, units],
+                in_=w1_grouped[:, two * 2 * P * PACK : (two + 1) * 2 * P * PACK],
+            )
+
+        w2_grouped = keep.tile([P, PASSES, OUT, PACK], BF16, align_bytes=64)
+        w2_codes = keep.tile([P, PASSES, OUT], U32, align_bytes=64)
+        w2_scales = keep.tile([P, PASSES, OUT], U8, align_bytes=64)
+
+        def quantise_w2():
+            for g in range(PASSES):
+                w2_flip = y_psum.tile([P, PACK, OUT], BF16, tag="y_sums")
+                for t in range(PACK):
+                    for a in range(O_TILES):
+                        first = (g * PACK + t) * P
+                        nc.tensor.transpose(
+                            w2_flip[:, t, a * P : (a + 1) * P],
+                            w2_rows[:, a, first : first + P],
+                            identity_bf16[:],
+                        )
+                nc.scalar.copy(
+                    out=w2_grouped[:, g, :, :], in_=w2_flip[:].rearrange("r t o -> r o t")
+                )
+            nc.vector.quantize_mx(
+                out=w2_codes[:].rearrange("r g o -> r (g o)").bitcast(FP8X4),
+                scales=w2_scales[:].rearrange("r g o -> r (g o)"),
+                in_=w2_grouped[:].rearrange("r g o t -> r (g o t)"),
+            )
 
         x_grouped = {}
         x_codes = {}
@@ -148,17 +204,19 @@ def tile_edgenetwork_t_kernel(
 
         terms = {}
 
-        def unquantised_term(pair):
-            for j in range(M_TILES):
-                terms[pair, j] = term_pool.tile([P, PAIR], F32, name="term")
+        def unquantised_term(c, n_chunks, g):
+            for j in range(g * PACK, (g + 1) * PACK):
+                term = term_pool.tile([P, n_chunks * CHUNK], F32, name="term")
                 nc.gpsimd.tensor_scalar(
-                    out=terms[pair, j][:],
-                    in0=edge_all[:, pair * PAIR : (pair + 1) * PAIR],
-                    scalar1=w1_edge[:, j : j + 1],
+                    out=term[:],
+                    in0=edge_all[:, c * CHUNK : (c + n_chunks) * CHUNK],
+                    scalar1=w1_edge[j // PACK][:, j % PACK : j % PACK + 1],
                     scalar2=bias_cols[:, j : j + 1],
                     op0=MULT,
                     op1=ADD,
                 )
+                for i in range(n_chunks):
+                    terms[c + i, j] = term[:, i * CHUNK : (i + 1) * CHUNK]
 
         pre = {}
         h_grouped = {}
@@ -179,13 +237,7 @@ def tile_edgenetwork_t_kernel(
                     start=True,
                     stop=True,
                 )
-                first = (c % 2) * CHUNK
-                nc.vector.tensor_tensor(
-                    out=pre[c, g][:, t, :],
-                    in0=sums[:],
-                    in1=terms[c // 2, j][:, first : first + CHUNK],
-                    op=ADD,
-                )
+                nc.vector.tensor_tensor(out=pre[c, g][:, t, :], in0=sums[:], in1=terms[c, j], op=ADD)
 
         def rectify(c, g):
             h_grouped[c, g] = h_pool.tile([P, CHUNK, PACK], BF16, align_bytes=64, name="h_grouped")
@@ -205,17 +257,15 @@ def tile_edgenetwork_t_kernel(
                 in_=h_grouped[c, g][:].rearrange("r e t -> r (e t)"),
             )
 
-        out_dram = out.rearrange("(b r) o -> r b o", r=P)
-
         y_flipped = {}
 
         def second_matmul(c):
             y_flipped[c] = yt_pool.tile([P, O_TILES, CHUNK], F32, name="y_flipped")
-            for a in range(O_TILES):
-                y_sums = y_psum.tile([P, CHUNK], F32, tag="y_sums")
-                for g in range(PASSES):
+            y_sums = [y_psum.tile([P, CHUNK], F32, tag="y_sums", name="y_sums") for a in range(O_TILES)]
+            for g in range(PASSES):
+                for a in range(O_TILES):
                     nc.tensor.matmul_mx(
-                        out=y_sums[:],
+                        out=y_sums[a][:],
                         lhsT=w2_codes[:, g, a * P : (a + 1) * P].bitcast(FP8X4),
                         lhsT_scale=w2_scales[:, g, a * P : (a + 1) * P],
                         rhs=h_codes[c][:, g, :].bitcast(FP8X4),
@@ -223,15 +273,18 @@ def tile_edgenetwork_t_kernel(
                         start=(g == 0),
                         stop=(g == PASSES - 1),
                     )
+            for a in range(O_TILES):
                 nc.scalar.activation(
                     out=y_flipped[c][:, a, :],
-                    in_=y_sums[:],
+                    in_=y_sums[a][:],
                     func=TANH,
                     bias=bias_cols[:, M_TILES + a : M_TILES + a + 1],
                 )
 
+        out_dram = out.rearrange("(b r) o -> r b o", r=P)
+
         def store_result(c):
-            for two in range(BLOCKS // 2):
+            for two, copy in enumerate((nc.vector.tensor_copy, nc.scalar.copy)):
                 y_flip = flip_psum.tile([P, 2, OUT], F32, tag="flip")
                 for i in range(2):
                     edges = slice((2 * two + i) * P, (2 * two + i + 1) * P)
@@ -240,82 +293,35 @@ def tile_edgenetwork_t_kernel(
                             y_flip[:, i, a * P : (a + 1) * P], y_flipped[c][:, a, edges], identity_f32[:]
                         )
                 y = y_pool.tile([P, 2, OUT], F32, name="y")
-                nc.scalar.copy(out=y[:], in_=y_flip[:])
+                copy(out=y[:], in_=y_flip[:])
                 first = c * BLOCKS + 2 * two
                 nc.sync.dma_start(out=out_dram[:, first : first + 2, :], in_=y[:])
 
-        bias_flip = y_psum.tile([P, P], BF16, tag="y_sums")
-        nc.tensor.transpose(bias_flip[:], bias_rows[:], identity_bf16[:])
-        bias_cols = keep.tile([P, M_TILES + O_TILES], F32)
-        nc.vector.tensor_copy(out=bias_cols[:], in_=bias_flip[:, 0 : M_TILES + O_TILES])
-
-        w1_words = w1_rows[:].bitcast(F32)
-        w1_edge = keep.tile([P, M_TILES], F32)
-        w1_grouped = keep.tile([P, MID * PACK], BF16, align_bytes=64)
-        w1_codes = keep.tile([P, MID], U32, align_bytes=64)
-        w1_scales = keep.tile([P, MID], U8, align_bytes=64)
-
-        def quantise_w1(two):
-            units = slice(two * 2 * P, (two + 1) * 2 * P)
-            nc.vector.quantize_mx(
-                out=w1_codes[:, units].bitcast(FP8X4),
-                scales=w1_scales[:, units],
-                in_=w1_grouped[:, two * 2 * P * PACK : (two + 1) * 2 * P * PACK],
-            )
-
-        def flip_w1(two):
-            tiles = slice(2 * two, 2 * two + 2)
-            nc.vector.tensor_copy(out=w1_edge[:, tiles], in_=w1_rows[:, tiles, NODE])
-            w1_flip = h_psum.tile([P, 2, 2, P], F32, tag="sums")
-            transpose_words(nc, w1_flip, w1_words[:, tiles, :], identity_f32[:])
-            nc.vector.tensor_copy(
-                out=grouped_words(w1_grouped[:])[:, tiles, :, :],
-                in_=w1_flip[:].rearrange("q b u r -> q b r u"),
-            )
-
-        flip_w1(0)
-        flip_w1(1)
-        quantise_w1(0)
         flip_x(0)
-        quantise_w1(1)
-        quantise_x(0)
-        flip_w1(2)
-        flip_w1(3)
-        quantise_w1(2)
-        quantise_w1(3)
-        unquantised_term(0)
-
-        w2_grouped = keep.tile([P, PASSES, OUT, PACK], BF16, align_bytes=64)
-        w2_codes = keep.tile([P, PASSES, OUT], U32, align_bytes=64)
-        w2_scales = keep.tile([P, PASSES, OUT], U8, align_bytes=64)
-
-        def quantise_w2():
-            for g in range(PASSES):
-                w2_flip = y_psum.tile([P, PACK, OUT], BF16, tag="y_sums")
-                for t in range(PACK):
-                    for a in range(O_TILES):
-                        first = (g * PACK + t) * P
-                        nc.tensor.transpose(
-                            w2_flip[:, t, a * P : (a + 1) * P],
-                            w2_rows[:, a, first : first + P],
-                            identity_bf16[:],
-                        )
-                nc.scalar.copy(
-                    out=w2_grouped[:, g, :, :], in_=w2_flip[:].rearrange("r t o -> r o t")
-                )
-            nc.vector.quantize_mx(
-                out=w2_codes[:].rearrange("r g o -> r (g o)").bitcast(FP8X4),
-                scales=w2_scales[:].rearrange("r g o -> r (g o)"),
-                in_=w2_grouped[:].rearrange("r g o t -> r (g o t)"),
-            )
+        for two in range(2):
+            flip_w1(two, h_psum.tile([P, 2, 2, P], F32, tag="sums", name="w1_flip"), nc.vector.tensor_copy)
+            quantise_w1(two)
+            if two == 0:
+                quantise_x(0)
+        unquantised_term(0, 1, 0)
 
         for c in range(N_CHUNKS + 2):
             if c < N_CHUNKS:
                 project(c, 0)
+            if c == 0:
+                for two in range(2, 4):
+                    flip_w1(two, y_psum.tile([P, 2, 2, P], F32, tag="y_sums", name="w1_flip"), nc.scalar.copy)
+                unquantised_term(0, 1, 1)
+                unquantised_term(1, 1, 0)
+                unquantised_term(1, 1, 1)
             if c + 1 < N_CHUNKS:
                 flip_x(c + 1)
-            if c % 2 == 0 and c // 2 + 1 < N_CHUNKS // 2:
-                unquantised_term(c // 2 + 1)
+            if c % 2 == 0 and c + 2 < N_CHUNKS:
+                unquantised_term(c + 2, 2, 0)
+                unquantised_term(c + 2, 2, 1)
+            if c == 0:
+                quantise_w1(2)
+                quantise_w1(3)
             if 1 <= c <= N_CHUNKS:
                 quantise_h(c - 1, 1)
             if c + 1 < N_CHUNKS:
@@ -325,11 +331,10 @@ def tile_edgenetwork_t_kernel(
                 project(c, 1)
             if c == 0:
                 quantise_w2()
+            if c >= 2:
+                store_result(c - 2)
             if 1 <= c <= N_CHUNKS:
                 second_matmul(c - 1)
             if c < N_CHUNKS:
                 quantise_h(c, 0)
-            if c >= 2:
-                store_result(c - 2)
-            if c < N_CHUNKS:
                 rectify(c, 1)

@@ -25,6 +25,7 @@ N_CHUNKS = EDGES // CHUNK
 M_TILES = MID // P
 PASSES = M_TILES // PACK
 O_TILES = OUT // P
+SLOTS = N_CHUNKS * PASSES
 W1_PITCH = NODE + 16
 
 
@@ -56,8 +57,8 @@ def tile_edgenetwork_t_kernel(
         keep = ctx.enter_context(tc.tile_pool(name="keep", bufs=1))
         x_pool = ctx.enter_context(tc.tile_pool(name="x_rows", bufs=N_CHUNKS))
         xq_pool = ctx.enter_context(tc.tile_pool(name="x_quantised", bufs=2))
-        term_pool = ctx.enter_context(tc.tile_pool(name="term", bufs=2 * M_TILES))
-        h_pool = ctx.enter_context(tc.tile_pool(name="hidden", bufs=3))
+        term_pool = ctx.enter_context(tc.tile_pool(name="term", bufs=6))
+        h_pool = ctx.enter_context(tc.tile_pool(name="hidden", bufs=4))
         hq_pool = ctx.enter_context(tc.tile_pool(name="hidden_quantised", bufs=2))
         yt_pool = ctx.enter_context(tc.tile_pool(name="result_flipped", bufs=3))
         y_pool = ctx.enter_context(tc.tile_pool(name="result", bufs=4))
@@ -128,19 +129,16 @@ def tile_edgenetwork_t_kernel(
 
         bias_flip = y_psum.tile([P, P], BF16, tag="y_sums")
         nc.tensor.transpose(bias_flip[:], bias_rows[:], identity_bf16[:])
-        bias_cols = keep.tile([P, M_TILES + O_TILES], F32)
+        bias_cols = keep.tile([P, M_TILES + O_TILES], BF16)
         nc.vector.tensor_copy(out=bias_cols[:], in_=bias_flip[:, 0 : M_TILES + O_TILES])
 
         w1_words = w1_rows[:].bitcast(F32)
-        w1_edge = [keep.tile([P, PACK], F32, name="w1_edge_%d" % g) for g in range(PASSES)]
         w1_grouped = keep.tile([P, MID * PACK], BF16, align_bytes=64)
         w1_codes = keep.tile([P, MID], U32, align_bytes=64)
         w1_scales = keep.tile([P, MID], U8, align_bytes=64)
 
         def flip_w1(two, bank, copy):
             tiles = slice(2 * two, 2 * two + 2)
-            first = (2 * two) % PACK
-            copy(out=w1_edge[2 * two // PACK][:, first : first + 2], in_=w1_rows[:, tiles, NODE])
             transpose_words(nc, bank, w1_words[:, tiles, :], identity_f32[:])
             copy(
                 out=grouped_words(w1_grouped[:])[:, tiles, :, :],
@@ -159,7 +157,7 @@ def tile_edgenetwork_t_kernel(
         w2_codes = keep.tile([P, PASSES, OUT], U32, align_bytes=64)
         w2_scales = keep.tile([P, PASSES, OUT], U8, align_bytes=64)
 
-        def quantise_w2():
+        def flip_w2():
             for g in range(PASSES):
                 w2_flip = y_psum.tile([P, PACK, OUT], BF16, tag="y_sums")
                 for t in range(PACK):
@@ -173,6 +171,8 @@ def tile_edgenetwork_t_kernel(
                 nc.scalar.copy(
                     out=w2_grouped[:, g, :, :], in_=w2_flip[:].rearrange("r t o -> r o t")
                 )
+
+        def quantise_w2():
             nc.vector.quantize_mx(
                 out=w2_codes[:].rearrange("r g o -> r (g o)").bitcast(FP8X4),
                 scales=w2_scales[:].rearrange("r g o -> r (g o)"),
@@ -183,17 +183,16 @@ def tile_edgenetwork_t_kernel(
         x_codes = {}
         x_scales = {}
 
-        def flip_x(c):
-            words = x_rows[c][:].bitcast(F32)
-            x_grouped[c] = xq_pool.tile([P, CHUNK * PACK], BF16, align_bytes=64, name="x_grouped")
-            for two in range(BLOCKS // 2):
-                blocks = slice(2 * two, 2 * two + 2)
-                x_flip = flip_psum.tile([P, 2, 2, P], F32, tag="flip")
-                transpose_words(nc, x_flip, words[:, blocks, :], identity_f32[:])
-                nc.scalar.copy(
-                    out=grouped_words(x_grouped[c][:])[:, blocks, :, :],
-                    in_=x_flip[:].rearrange("q b u r -> q b r u"),
-                )
+        def flip_x(c, two):
+            if two == 0:
+                x_grouped[c] = xq_pool.tile([P, CHUNK * PACK], BF16, align_bytes=64, name="x_grouped")
+            blocks = slice(2 * two, 2 * two + 2)
+            x_flip = flip_psum.tile([P, 2, 2, P], F32, tag="flip")
+            transpose_words(nc, x_flip, x_rows[c][:].bitcast(F32)[:, blocks, :], identity_f32[:])
+            nc.scalar.copy(
+                out=grouped_words(x_grouped[c][:])[:, blocks, :, :],
+                in_=x_flip[:].rearrange("q b u r -> q b r u"),
+            )
 
         def quantise_x(c):
             x_codes[c] = xq_pool.tile([P, CHUNK], U32, align_bytes=64, name="x_codes")
@@ -204,137 +203,175 @@ def tile_edgenetwork_t_kernel(
 
         terms = {}
 
-        def unquantised_term(c, n_chunks, g):
-            for j in range(g * PACK, (g + 1) * PACK):
-                term = term_pool.tile([P, n_chunks * CHUNK], F32, name="term")
+        def unquantised_term(i):
+            c, g = divmod(i, PASSES)
+            terms[i] = term_pool.tile([P, PACK, CHUNK], F32, name="term")
+            for t in range(PACK):
+                j = g * PACK + t
                 nc.gpsimd.tensor_scalar(
-                    out=term[:],
-                    in0=edge_all[:, c * CHUNK : (c + n_chunks) * CHUNK],
-                    scalar1=w1_edge[j // PACK][:, j % PACK : j % PACK + 1],
+                    out=terms[i][:, t, :],
+                    in0=edge_all[:, c * CHUNK : (c + 1) * CHUNK],
+                    scalar1=w1_rows[:, j, NODE : NODE + 1],
                     scalar2=bias_cols[:, j : j + 1],
                     op0=MULT,
                     op1=ADD,
                 )
-                for i in range(n_chunks):
-                    terms[c + i, j] = term[:, i * CHUNK : (i + 1) * CHUNK]
 
-        pre = {}
+        sums = {}
         h_grouped = {}
         h_codes = {}
         h_scales = {}
 
-        def project(c, g):
-            pre[c, g] = h_pool.tile([P, PACK, CHUNK], BF16, name="pre")
-            for t in range(PACK):
-                j = g * PACK + t
-                sums = h_psum.tile([P, CHUNK], F32, tag="sums")
-                nc.tensor.matmul_mx(
-                    out=sums[:],
-                    lhsT=w1_codes[:, j * P : (j + 1) * P].bitcast(FP8X4),
-                    lhsT_scale=w1_scales[:, j * P : (j + 1) * P],
-                    rhs=x_codes[c][:].bitcast(FP8X4),
-                    rhs_scale=x_scales[c][:],
-                    start=True,
-                    stop=True,
-                )
-                nc.vector.tensor_tensor(out=pre[c, g][:, t, :], in0=sums[:], in1=terms[c, j], op=ADD)
+        def first_matmul(i):
+            c, g = divmod(i, PASSES)
+            for b in range(BLOCKS):
+                edges = slice(b * P, (b + 1) * P)
+                sums[i, b] = h_psum.tile([P, PACK, P], F32, tag="sums", name="sums")
+                for t in range(PACK):
+                    j = g * PACK + t
+                    nc.tensor.matmul_mx(
+                        out=sums[i, b][:, t, :],
+                        lhsT=w1_codes[:, j * P : (j + 1) * P].bitcast(FP8X4),
+                        lhsT_scale=w1_scales[:, j * P : (j + 1) * P],
+                        rhs=x_codes[c][:, edges].bitcast(FP8X4),
+                        rhs_scale=x_scales[c][:, edges],
+                        start=True,
+                        stop=True,
+                    )
 
-        def rectify(c, g):
-            h_grouped[c, g] = h_pool.tile([P, CHUNK, PACK], BF16, align_bytes=64, name="h_grouped")
-            nc.scalar.activation(
-                out=h_grouped[c, g][:].rearrange("r (n i) t -> r n t i", i=PACK),
-                in_=pre[c, g][:].rearrange("r t (n i) -> r n t i", i=PACK),
-                func=RELU,
+        def add_term(i, b):
+            if b == 0:
+                h_grouped[i] = h_pool.tile([P, CHUNK, PACK], BF16, align_bytes=64, name="h_grouped")
+            edges = slice(b * P, (b + 1) * P)
+            nc.vector.tensor_tensor(
+                out=h_grouped[i][:, edges, :].rearrange("r (n i) t -> r n t i", i=PACK),
+                in0=sums[i, b][:].rearrange("r t (n i) -> r n t i", i=PACK),
+                in1=terms[i][:, :, edges].rearrange("r t (n i) -> r n t i", i=PACK),
+                op=ADD,
             )
 
-        def quantise_h(c, g):
+        def rectify_vector(i, first, last):
+            block = h_grouped[i][:, first * P : last * P, :]
+            nc.vector.tensor_scalar_max(block, block, 0.0)
+
+        def rectify_scalar(i, first, last):
+            block = h_grouped[i][:, first * P : last * P, :]
+            nc.scalar.activation(out=block, in_=block, func=RELU)
+
+        def quantise_h(i):
+            c, g = divmod(i, PASSES)
             if g == 0:
                 h_codes[c] = hq_pool.tile([P, PASSES, CHUNK], U32, align_bytes=64, name="h_codes")
                 h_scales[c] = hq_pool.tile([P, PASSES, CHUNK], U8, align_bytes=64, name="h_scales")
             nc.vector.quantize_mx(
                 out=h_codes[c][:, g, :].bitcast(FP8X4),
                 scales=h_scales[c][:, g, :],
-                in_=h_grouped[c, g][:].rearrange("r e t -> r (e t)"),
+                in_=h_grouped[i][:].rearrange("r e t -> r (e t)"),
             )
 
+        y_sums = {}
         y_flipped = {}
 
-        def second_matmul(c):
-            y_flipped[c] = yt_pool.tile([P, O_TILES, CHUNK], F32, name="y_flipped")
-            y_sums = [y_psum.tile([P, CHUNK], F32, tag="y_sums", name="y_sums") for a in range(O_TILES)]
-            for g in range(PASSES):
-                for a in range(O_TILES):
-                    nc.tensor.matmul_mx(
-                        out=y_sums[a][:],
-                        lhsT=w2_codes[:, g, a * P : (a + 1) * P].bitcast(FP8X4),
-                        lhsT_scale=w2_scales[:, g, a * P : (a + 1) * P],
-                        rhs=h_codes[c][:, g, :].bitcast(FP8X4),
-                        rhs_scale=h_scales[c][:, g, :],
-                        start=(g == 0),
-                        stop=(g == PASSES - 1),
-                    )
+        def second_matmul(i):
+            c, g = divmod(i, PASSES)
             for a in range(O_TILES):
-                nc.scalar.activation(
-                    out=y_flipped[c][:, a, :],
-                    in_=y_sums[a][:],
-                    func=TANH,
-                    bias=bias_cols[:, M_TILES + a : M_TILES + a + 1],
+                if g == 0:
+                    y_sums[c, a] = y_psum.tile([P, CHUNK], F32, tag="y_sums", name="y_sums")
+                nc.tensor.matmul_mx(
+                    out=y_sums[c, a][:],
+                    lhsT=w2_codes[:, g, a * P : (a + 1) * P].bitcast(FP8X4),
+                    lhsT_scale=w2_scales[:, g, a * P : (a + 1) * P],
+                    rhs=h_codes[c][:, g, :].bitcast(FP8X4),
+                    rhs_scale=h_scales[c][:, g, :],
+                    start=(g == 0),
+                    stop=(g == PASSES - 1),
                 )
+
+        def activate(c, a):
+            if a == 0:
+                y_flipped[c] = yt_pool.tile([P, O_TILES, CHUNK], F32, name="y_flipped")
+            nc.scalar.activation(
+                out=y_flipped[c][:, a, :],
+                in_=y_sums[c, a][:],
+                func=TANH,
+                bias=bias_cols[:, M_TILES + a : M_TILES + a + 1],
+            )
 
         out_dram = out.rearrange("(b r) o -> r b o", r=P)
 
-        def store_result(c):
-            for two, copy in enumerate((nc.vector.tensor_copy, nc.scalar.copy)):
-                y_flip = flip_psum.tile([P, 2, OUT], F32, tag="flip")
-                for i in range(2):
-                    edges = slice((2 * two + i) * P, (2 * two + i + 1) * P)
-                    for a in range(O_TILES):
-                        nc.tensor.transpose(
-                            y_flip[:, i, a * P : (a + 1) * P], y_flipped[c][:, a, edges], identity_f32[:]
-                        )
-                y = y_pool.tile([P, 2, OUT], F32, name="y")
-                copy(out=y[:], in_=y_flip[:])
-                first = c * BLOCKS + 2 * two
-                nc.sync.dma_start(out=out_dram[:, first : first + 2, :], in_=y[:])
+        def store_result(c, two, copy):
+            y_flip = flip_psum.tile([P, 2, OUT], F32, tag="flip")
+            for i in range(2):
+                edges = slice((2 * two + i) * P, (2 * two + i + 1) * P)
+                for a in range(O_TILES):
+                    nc.tensor.transpose(
+                        y_flip[:, i, a * P : (a + 1) * P], y_flipped[c][:, a, edges], identity_f32[:]
+                    )
+            y = y_pool.tile([P, 2, OUT], F32, name="y")
+            copy(out=y[:], in_=y_flip[:])
+            first = c * BLOCKS + 2 * two
+            nc.sync.dma_start(out=out_dram[:, first : first + 2, :], in_=y[:])
 
-        flip_x(0)
+        for two in range(2):
+            flip_x(0, two)
         for two in range(2):
             flip_w1(two, h_psum.tile([P, 2, 2, P], F32, tag="sums", name="w1_flip"), nc.vector.tensor_copy)
             quantise_w1(two)
             if two == 0:
                 quantise_x(0)
-        unquantised_term(0, 1, 0)
+        for i in range(3):
+            unquantised_term(i)
+        first_matmul(0)
 
-        for c in range(N_CHUNKS + 2):
-            if c < N_CHUNKS:
-                project(c, 0)
-            if c == 0:
+        last = N_CHUNKS - 1
+        for i in range(SLOTS + 3):
+            c, g = divmod(i, PASSES)
+            if i == 0:
                 for two in range(2, 4):
                     flip_w1(two, y_psum.tile([P, 2, 2, P], F32, tag="y_sums", name="w1_flip"), nc.scalar.copy)
-                unquantised_term(0, 1, 1)
-                unquantised_term(1, 1, 0)
-                unquantised_term(1, 1, 1)
-            if c + 1 < N_CHUNKS:
-                flip_x(c + 1)
-            if c % 2 == 0 and c + 2 < N_CHUNKS:
-                unquantised_term(c + 2, 2, 0)
-                unquantised_term(c + 2, 2, 1)
-            if c == 0:
-                quantise_w1(2)
-                quantise_w1(3)
-            if 1 <= c <= N_CHUNKS:
-                quantise_h(c - 1, 1)
-            if c + 1 < N_CHUNKS:
-                quantise_x(c + 1)
-            if c < N_CHUNKS:
-                rectify(c, 0)
-                project(c, 1)
-            if c == 0:
+                for two in range(2):
+                    flip_x(1, two)
+            elif g == 0:
+                if 0 <= c - 2 < last:
+                    activate(c - 2, 1)
+                if c + 1 < N_CHUNKS:
+                    flip_x(c + 1, 1)
+                if 0 <= c - 3:
+                    store_result(c - 3, 1, nc.scalar.copy)
+                if 0 <= c - 1 < N_CHUNKS:
+                    second_matmul(i - 2)
+            else:
+                if 0 <= c - 1 < N_CHUNKS:
+                    second_matmul(i - 2)
+                if c + 2 < N_CHUNKS:
+                    flip_x(c + 2, 0)
+                if 0 <= c - 2 < N_CHUNKS:
+                    store_result(c - 2, 0, nc.scalar.copy)
+                if 0 <= c - 1 < N_CHUNKS:
+                    activate(c - 1, 0)
+                if c - 1 == last:
+                    activate(last, 1)
+            if i == 1:
+                flip_w2()
+            if i + 3 < SLOTS:
+                unquantised_term(i + 3)
+            if i < SLOTS:
+                add_term(i, 0)
+                add_term(i, 1)
+                if i == 0:
+                    quantise_w1(2)
+                    quantise_w1(3)
+                rectify_vector(i, 0, 1)
+                add_term(i, 2)
+                add_term(i, 3)
+                rectify_scalar(i, 1, BLOCKS)
+            if 1 <= i <= SLOTS:
+                quantise_h(i - 1)
+            if i == 1:
                 quantise_w2()
-            if c >= 2:
-                store_result(c - 2)
-            if 1 <= c <= N_CHUNKS:
-                second_matmul(c - 1)
-            if c < N_CHUNKS:
-                quantise_h(c, 0)
-                rectify(c, 1)
+            if g == 0 and c + 1 < N_CHUNKS:
+                quantise_x(c + 1)
+            if i + 1 < SLOTS:
+                first_matmul(i + 1)
+        store_result(last, 0, nc.scalar.copy)
+        store_result(last, 1, nc.vector.tensor_copy)

@@ -57,7 +57,7 @@ def tile_edgenetwork_t_kernel(
         keep = ctx.enter_context(tc.tile_pool(name="keep", bufs=1))
         x_pool = ctx.enter_context(tc.tile_pool(name="x_rows", bufs=N_CHUNKS))
         xq_pool = ctx.enter_context(tc.tile_pool(name="x_quantised", bufs=2))
-        term_pool = ctx.enter_context(tc.tile_pool(name="term", bufs=6))
+        term_pool = ctx.enter_context(tc.tile_pool(name="term", bufs=4))
         h_pool = ctx.enter_context(tc.tile_pool(name="hidden", bufs=4))
         hq_pool = ctx.enter_context(tc.tile_pool(name="hidden_quantised", bufs=2))
         yt_pool = ctx.enter_context(tc.tile_pool(name="result_flipped", bufs=3))
@@ -203,19 +203,20 @@ def tile_edgenetwork_t_kernel(
 
         terms = {}
 
-        def unquantised_term(i):
-            c, g = divmod(i, PASSES)
-            terms[i] = term_pool.tile([P, PACK, CHUNK], F32, name="term")
+        def unquantised_term(c, n_chunks, g):
+            term = term_pool.tile([P, PACK, n_chunks * CHUNK], F32, name="term")
             for t in range(PACK):
                 j = g * PACK + t
                 nc.gpsimd.tensor_scalar(
-                    out=terms[i][:, t, :],
-                    in0=edge_all[:, c * CHUNK : (c + 1) * CHUNK],
+                    out=term[:, t, :],
+                    in0=edge_all[:, c * CHUNK : (c + n_chunks) * CHUNK],
                     scalar1=w1_rows[:, j, NODE : NODE + 1],
                     scalar2=bias_cols[:, j : j + 1],
                     op0=MULT,
                     op1=ADD,
                 )
+            for k in range(n_chunks):
+                terms[(c + k) * PASSES + g] = term[:, :, k * CHUNK : (k + 1) * CHUNK]
 
         sums = {}
         h_grouped = {}
@@ -319,8 +320,8 @@ def tile_edgenetwork_t_kernel(
             quantise_w1(two)
             if two == 0:
                 quantise_x(0)
-        for i in range(3):
-            unquantised_term(i)
+        for i in range(2 * PASSES):
+            unquantised_term(i // PASSES, 1, i % PASSES)
         first_matmul(0)
 
         last = N_CHUNKS - 1
@@ -353,8 +354,6 @@ def tile_edgenetwork_t_kernel(
                     activate(last, 1)
             if i == 1:
                 flip_w2()
-            if i + 3 < SLOTS:
-                unquantised_term(i + 3)
             if i < SLOTS:
                 add_term(i, 0)
                 add_term(i, 1)
@@ -373,5 +372,10 @@ def tile_edgenetwork_t_kernel(
                 quantise_x(c + 1)
             if i + 1 < SLOTS:
                 first_matmul(i + 1)
+            if i < 2 * PASSES:
+                pair = 2 if i < PASSES else 4
+                unquantised_term(pair, 2, g)
+            elif 3 * PASSES <= i < 4 * PASSES:
+                unquantised_term(6, 2, g)
         store_result(last, 0, nc.scalar.copy)
         store_result(last, 1, nc.vector.tensor_copy)

@@ -12,6 +12,7 @@ ADD = mybir.AluOpType.add
 MULT = mybir.AluOpType.mult
 RELU = mybir.ActivationFunctionType.Relu
 TANH = mybir.ActivationFunctionType.Tanh
+IDENTITY = mybir.ActivationFunctionType.Identity
 
 P = 128
 PACK = 4
@@ -108,13 +109,13 @@ def tile_edgenetwork_t_kernel(
         nc.sync.dma_start(
             out=bias_rows[M_TILES : M_TILES + O_TILES, :], in_=b2.rearrange("(a r) -> a r", r=P)
         )
-        load_x(0)
         load_w1(0)
         load_edge(0, 1)
+        load_x(0)
         load_w1(1)
-        load_edge(1, 1)
         load_w1(2)
         load_w1(3)
+        load_edge(1, 1)
         load_x(1)
         nc.sync.dma_start(out=w2_rows[:], in_=W2.rearrange("(a r) m -> r a m", r=P))
         for c in range(2, N_CHUNKS):
@@ -194,11 +195,15 @@ def tile_edgenetwork_t_kernel(
                 in_=x_flip[:].rearrange("q b u r -> q b r u"),
             )
 
-        def quantise_x(c):
-            x_codes[c] = xq_pool.tile([P, CHUNK], U32, align_bytes=64, name="x_codes")
-            x_scales[c] = xq_pool.tile([P, CHUNK], U8, align_bytes=64, name="x_scales")
+        def quantise_x(c, first, last):
+            if first == 0:
+                x_codes[c] = xq_pool.tile([P, CHUNK], U32, align_bytes=64, name="x_codes")
+                x_scales[c] = xq_pool.tile([P, CHUNK], U8, align_bytes=64, name="x_scales")
+            edges = slice(first * P, last * P)
             nc.vector.quantize_mx(
-                out=x_codes[c][:].bitcast(FP8X4), scales=x_scales[c][:], in_=x_grouped[c][:]
+                out=x_codes[c][:, edges].bitcast(FP8X4),
+                scales=x_scales[c][:, edges],
+                in_=x_grouped[c][:, first * P * PACK : last * P * PACK],
             )
 
         terms = {}
@@ -217,6 +222,31 @@ def tile_edgenetwork_t_kernel(
                 )
             for k in range(n_chunks):
                 terms[(c + k) * PASSES + g] = term[:, :, k * CHUNK : (k + 1) * CHUNK]
+
+        w1_edge = keep.tile([P, PACK], F32)
+
+        def first_terms_vector():
+            terms[0] = term_pool.tile([P, PACK, CHUNK], F32, name="term")
+            for t in range(PACK):
+                nc.vector.tensor_scalar(
+                    out=terms[0][:, t, :],
+                    in0=edge_all[:, 0:CHUNK],
+                    scalar1=w1_rows[:, t, NODE : NODE + 1],
+                    scalar2=bias_cols[:, t : t + 1],
+                    op0=MULT,
+                    op1=ADD,
+                )
+
+        def first_terms_scalar():
+            terms[1] = term_pool.tile([P, PACK, CHUNK], F32, name="term")
+            for t in range(PACK):
+                nc.scalar.activation(
+                    out=terms[1][:, t, :],
+                    in_=edge_all[:, 0:CHUNK],
+                    func=IDENTITY,
+                    scale=w1_edge[:, t : t + 1],
+                    bias=bias_cols[:, PACK + t : PACK + t + 1],
+                )
 
         sums = {}
         h_grouped = {}
@@ -259,15 +289,16 @@ def tile_edgenetwork_t_kernel(
             block = h_grouped[i][:, first * P : last * P, :]
             nc.scalar.activation(out=block, in_=block, func=RELU)
 
-        def quantise_h(i):
+        def quantise_h(i, first, last):
             c, g = divmod(i, PASSES)
-            if g == 0:
+            edges = slice(first * P, last * P)
+            if g == 0 and first == 0:
                 h_codes[c] = hq_pool.tile([P, PASSES, CHUNK], U32, align_bytes=64, name="h_codes")
                 h_scales[c] = hq_pool.tile([P, PASSES, CHUNK], U8, align_bytes=64, name="h_scales")
             nc.vector.quantize_mx(
-                out=h_codes[c][:, g, :].bitcast(FP8X4),
-                scales=h_scales[c][:, g, :],
-                in_=h_grouped[i][:].rearrange("r e t -> r (e t)"),
+                out=h_codes[c][:, g, edges].bitcast(FP8X4),
+                scales=h_scales[c][:, g, edges],
+                in_=h_grouped[i][:, edges, :].rearrange("r e t -> r (e t)"),
             )
 
         y_sums = {}
@@ -298,6 +329,31 @@ def tile_edgenetwork_t_kernel(
                 bias=bias_cols[:, M_TILES + a : M_TILES + a + 1],
             )
 
+        def finish_half(c, two):
+            if two == 0:
+                y_flipped[c] = yt_pool.tile([P, O_TILES, CHUNK], F32, name="y_flipped")
+            half = CHUNK // 2
+            edges = slice(two * half, (two + 1) * half)
+            bank = h_psum.tile([P, O_TILES, half], F32, tag="sums", name="y_half")
+            for a in range(O_TILES):
+                for g in range(PASSES):
+                    nc.tensor.matmul_mx(
+                        out=bank[:, a, :],
+                        lhsT=w2_codes[:, g, a * P : (a + 1) * P].bitcast(FP8X4),
+                        lhsT_scale=w2_scales[:, g, a * P : (a + 1) * P],
+                        rhs=h_codes[c][:, g, edges].bitcast(FP8X4),
+                        rhs_scale=h_scales[c][:, g, edges],
+                        start=(g == 0),
+                        stop=(g == PASSES - 1),
+                    )
+            for a in range(O_TILES):
+                nc.scalar.activation(
+                    out=y_flipped[c][:, a, edges],
+                    in_=bank[:, a, :],
+                    func=TANH,
+                    bias=bias_cols[:, M_TILES + a : M_TILES + a + 1],
+                )
+
         out_dram = out.rearrange("(b r) o -> r b o", r=P)
 
         def store_result(c, two, copy):
@@ -313,48 +369,52 @@ def tile_edgenetwork_t_kernel(
             first = c * BLOCKS + 2 * two
             nc.sync.dma_start(out=out_dram[:, first : first + 2, :], in_=y[:])
 
-        for two in range(2):
-            flip_x(0, two)
-        for two in range(2):
-            flip_w1(two, h_psum.tile([P, 2, 2, P], F32, tag="sums", name="w1_flip"), nc.vector.tensor_copy)
-            quantise_w1(two)
-            if two == 0:
-                quantise_x(0)
-        for i in range(2 * PASSES):
-            unquantised_term(i // PASSES, 1, i % PASSES)
+        def w1_bank(pool, tag):
+            return pool.tile([P, 2, 2, P], F32, tag=tag, name="w1_flip")
+
+        flip_w1(0, w1_bank(h_psum, "sums"), nc.vector.tensor_copy)
+        quantise_w1(0)
+        flip_x(0, 0)
+        flip_x(0, 1)
+        first_terms_vector()
+        flip_w1(1, w1_bank(h_psum, "sums"), nc.vector.tensor_copy)
+        quantise_x(0, 0, 2)
+        quantise_w1(1)
+        quantise_x(0, 2, BLOCKS)
+        flip_w1(2, w1_bank(y_psum, "y_sums"), nc.scalar.copy)
+        flip_w1(3, w1_bank(y_psum, "y_sums"), nc.scalar.copy)
+        nc.vector.tensor_copy(out=w1_edge[:], in_=w1_rows[:, PACK:M_TILES, NODE])
+        first_terms_scalar()
+        for g in range(PASSES):
+            unquantised_term(1, 1, g)
         first_matmul(0)
 
         last = N_CHUNKS - 1
-        for i in range(SLOTS + 3):
+        for i in range(SLOTS):
             c, g = divmod(i, PASSES)
             if i == 0:
-                for two in range(2, 4):
-                    flip_w1(two, y_psum.tile([P, 2, 2, P], F32, tag="y_sums", name="w1_flip"), nc.scalar.copy)
                 for two in range(2):
                     flip_x(1, two)
             elif g == 0:
-                if 0 <= c - 2 < last:
+                if 0 <= c - 2:
                     activate(c - 2, 1)
                 if c + 1 < N_CHUNKS:
                     flip_x(c + 1, 1)
                 if 0 <= c - 3:
                     store_result(c - 3, 1, nc.scalar.copy)
-                if 0 <= c - 1 < N_CHUNKS:
-                    second_matmul(i - 2)
+                second_matmul(i - 2)
             else:
-                if 0 <= c - 1 < N_CHUNKS:
+                if 0 <= c - 1:
                     second_matmul(i - 2)
                 if c + 2 < N_CHUNKS:
                     flip_x(c + 2, 0)
-                if 0 <= c - 2 < N_CHUNKS:
+                if 0 <= c - 2:
                     store_result(c - 2, 0, nc.scalar.copy)
-                if 0 <= c - 1 < N_CHUNKS:
+                if 0 <= c - 1:
                     activate(c - 1, 0)
-                if c - 1 == last:
-                    activate(last, 1)
             if i == 1:
                 flip_w2()
-            if i < SLOTS:
+            if i < SLOTS - 1:
                 add_term(i, 0)
                 add_term(i, 1)
                 if i == 0:
@@ -364,18 +424,35 @@ def tile_edgenetwork_t_kernel(
                 add_term(i, 2)
                 add_term(i, 3)
                 rectify_scalar(i, 1, BLOCKS)
-            if 1 <= i <= SLOTS:
-                quantise_h(i - 1)
-            if i == 1:
-                quantise_w2()
-            if g == 0 and c + 1 < N_CHUNKS:
-                quantise_x(c + 1)
-            if i + 1 < SLOTS:
+                if 1 <= i:
+                    quantise_h(i - 1, 0, BLOCKS)
+                if i == 1:
+                    quantise_w2()
+                if g == 0 and c + 1 < N_CHUNKS:
+                    quantise_x(c + 1, 0, BLOCKS)
                 first_matmul(i + 1)
             if i < 2 * PASSES:
                 pair = 2 if i < PASSES else 4
                 unquantised_term(pair, 2, g)
             elif 3 * PASSES <= i < 4 * PASSES:
                 unquantised_term(6, 2, g)
+
+        i = SLOTS - 1
+        activate(last - 1, 1)
+        store_result(last - 2, 1, nc.scalar.copy)
+        add_term(i, 0)
+        add_term(i, 1)
+        rectify_vector(i, 0, 1)
+        add_term(i, 2)
+        rectify_vector(i, 1, 2)
+        quantise_h(i - 1, 0, BLOCKS)
+        add_term(i, 3)
+        quantise_h(i, 0, 2)
+        rectify_vector(i, 2, BLOCKS)
+        finish_half(last, 0)
+        quantise_h(i, 2, BLOCKS)
+        store_result(last - 1, 0, nc.vector.tensor_copy)
+        finish_half(last, 1)
+        store_result(last - 1, 1, nc.vector.tensor_copy)
         store_result(last, 0, nc.scalar.copy)
         store_result(last, 1, nc.vector.tensor_copy)

@@ -95,32 +95,29 @@ def tile_edgenetwork_t_kernel(
                 )
             x_rows.append(rows)
 
-        edge_all = keep.tile([P, EDGES], BF16)
-
-        def load_edge(c, n_chunks):
-            cols = slice(c * CHUNK, (c + n_chunks) * CHUNK)
-            nc.sync.dma_start(out=edge_all[:, cols], in_=edge_feat[cols].partition_broadcast(P))
-
         bias_rows = keep.tile([P, P], BF16)
         nc.vector.memset(bias_rows[:], 0.0)
+        edge_rows = keep.tile([P, CHUNK], BF16)
+        nc.vector.memset(edge_rows[:], 0.0)
+        edge_all = keep.tile([P, EDGES], BF16)
         w2_rows = keep.tile([P, O_TILES, MID], BF16)
 
         nc.sync.dma_start(out=bias_rows[0:M_TILES, :], in_=b1.rearrange("(j r) -> j r", r=P))
         nc.sync.dma_start(
             out=bias_rows[M_TILES : M_TILES + O_TILES, :], in_=b2.rearrange("(a r) -> a r", r=P)
         )
+        nc.sync.dma_start(out=edge_rows[0:N_CHUNKS, :], in_=edge_feat.rearrange("(c e) -> c e", e=CHUNK))
         load_w1(0)
-        load_edge(0, 1)
         load_x(0)
         load_w1(1)
         load_w1(2)
         load_w1(3)
-        load_edge(1, 1)
         load_x(1)
+        nc.sync.dma_start(
+            out=edge_all[:, 2 * CHUNK :], in_=edge_feat[2 * CHUNK : EDGES].partition_broadcast(P)
+        )
         nc.sync.dma_start(out=w2_rows[:], in_=W2.rearrange("(a r) m -> r a m", r=P))
         for c in range(2, N_CHUNKS):
-            if c % 2 == 0:
-                load_edge(c, 2)
             load_x(c)
 
         identity_bf16 = keep.tile([P, P], BF16)
@@ -132,6 +129,19 @@ def tile_edgenetwork_t_kernel(
         nc.tensor.transpose(bias_flip[:], bias_rows[:], identity_bf16[:])
         bias_cols = keep.tile([P, M_TILES + O_TILES], BF16)
         nc.vector.tensor_copy(out=bias_cols[:], in_=bias_flip[:, 0 : M_TILES + O_TILES])
+
+        def spread_edge(c, bank):
+            for k in range(2):
+                nc.tensor.matmul(
+                    bank[:, k, :],
+                    lhsT=identity_bf16[:, c + k : c + k + 1].to_broadcast([P, P]),
+                    rhs=edge_rows[:],
+                    start=True,
+                    stop=True,
+                )
+            nc.scalar.copy(
+                out=edge_all[:, c * CHUNK : (c + 2) * CHUNK], in_=bank[:].rearrange("p k e -> p (k e)")
+            )
 
         w1_words = w1_rows[:].bitcast(F32)
         w1_grouped = keep.tile([P, MID * PACK], BF16, align_bytes=64)
@@ -372,6 +382,10 @@ def tile_edgenetwork_t_kernel(
         def w1_bank(pool, tag):
             return pool.tile([P, 2, 2, P], F32, tag=tag, name="w1_flip")
 
+        def edge_bank(pool, tag):
+            return pool.tile([P, 2, CHUNK], BF16, tag=tag, name="edge_spread")
+
+        spread_edge(0, edge_bank(h_psum, "sums"))
         flip_w1(0, w1_bank(h_psum, "sums"), nc.vector.tensor_copy)
         quantise_w1(0)
         flip_x(0, 0)
@@ -395,7 +409,7 @@ def tile_edgenetwork_t_kernel(
             if i == 0:
                 for two in range(2):
                     flip_x(1, two)
-            elif g == 0:
+            if g == 0 and 1 <= c:
                 if 0 <= c - 2:
                     activate(c - 2, 1)
                 if c + 1 < N_CHUNKS:
@@ -403,7 +417,7 @@ def tile_edgenetwork_t_kernel(
                 if 0 <= c - 3:
                     store_result(c - 3, 1, nc.scalar.copy)
                 second_matmul(i - 2)
-            else:
+            if g == 1:
                 if 0 <= c - 1:
                     second_matmul(i - 2)
                 if c + 2 < N_CHUNKS:

@@ -60,7 +60,8 @@ def tile_edgenetwork_t_kernel(
         xq_pool = ctx.enter_context(tc.tile_pool(name="x_quantised", bufs=2))
         term_pool = ctx.enter_context(tc.tile_pool(name="term", bufs=4))
         h_pool = ctx.enter_context(tc.tile_pool(name="hidden", bufs=4))
-        hq_pool = ctx.enter_context(tc.tile_pool(name="hidden_quantised", bufs=2))
+        hq_pool = ctx.enter_context(tc.tile_pool(name="hidden_quantised", bufs=3))
+        joint_pool = ctx.enter_context(tc.tile_pool(name="joint", bufs=3))
         yt_pool = ctx.enter_context(tc.tile_pool(name="result_flipped", bufs=3))
         y_pool = ctx.enter_context(tc.tile_pool(name="result", bufs=4))
         flip_psum = ctx.enter_context(tc.psum_pool(name="flip", bufs=2))
@@ -113,11 +114,12 @@ def tile_edgenetwork_t_kernel(
         load_w1(2)
         load_w1(3)
         load_x(1)
+        load_x(2)
+        nc.sync.dma_start(out=w2_rows[:], in_=W2.rearrange("(a r) m -> r a m", r=P))
         nc.sync.dma_start(
             out=edge_all[:, 2 * CHUNK :], in_=edge_feat[2 * CHUNK : EDGES].partition_broadcast(P)
         )
-        nc.sync.dma_start(out=w2_rows[:], in_=W2.rearrange("(a r) m -> r a m", r=P))
-        for c in range(2, N_CHUNKS):
+        for c in range(3, N_CHUNKS):
             load_x(c)
 
         identity_bf16 = keep.tile([P, P], BF16)
@@ -195,20 +197,23 @@ def tile_edgenetwork_t_kernel(
         x_scales = {}
 
         def flip_x(c, two):
-            if two == 0:
-                x_grouped[c] = xq_pool.tile([P, CHUNK * PACK], BF16, align_bytes=64, name="x_grouped")
             blocks = slice(2 * two, 2 * two + 2)
             x_flip = flip_psum.tile([P, 2, 2, P], F32, tag="flip")
             transpose_words(nc, x_flip, x_rows[c][:].bitcast(F32)[:, blocks, :], identity_f32[:])
             nc.scalar.copy(
-                out=grouped_words(x_grouped[c][:])[:, blocks, :, :],
+                out=grouped_words(x_grouped[c])[:, blocks, :, :],
                 in_=x_flip[:].rearrange("q b u r -> q b r u"),
             )
 
+        def open_x(c):
+            grouped = xq_pool.tile([P, CHUNK * PACK], BF16, align_bytes=64, name="x_grouped")
+            codes = xq_pool.tile([P, CHUNK], U32, align_bytes=64, name="x_codes")
+            scales = xq_pool.tile([P, CHUNK], U8, align_bytes=64, name="x_scales")
+            x_grouped[c] = grouped[:, :]
+            x_codes[c] = codes[:, :]
+            x_scales[c] = scales[:, :]
+
         def quantise_x(c, first, last):
-            if first == 0:
-                x_codes[c] = xq_pool.tile([P, CHUNK], U32, align_bytes=64, name="x_codes")
-                x_scales[c] = xq_pool.tile([P, CHUNK], U8, align_bytes=64, name="x_scales")
             edges = slice(first * P, last * P)
             nc.vector.quantize_mx(
                 out=x_codes[c][:, edges].bitcast(FP8X4),
@@ -281,8 +286,9 @@ def tile_edgenetwork_t_kernel(
                     )
 
         def add_term(i, b):
-            if b == 0:
-                h_grouped[i] = h_pool.tile([P, CHUNK, PACK], BF16, align_bytes=64, name="h_grouped")
+            if b == 0 and i not in h_grouped:
+                h_tile = h_pool.tile([P, CHUNK, PACK], BF16, align_bytes=64, name="h_grouped")
+                h_grouped[i] = h_tile[:, :, :]
             edges = slice(b * P, (b + 1) * P)
             nc.vector.tensor_tensor(
                 out=h_grouped[i][:, edges, :].rearrange("r (n i) t -> r n t i", i=PACK),
@@ -300,16 +306,35 @@ def tile_edgenetwork_t_kernel(
             nc.scalar.activation(out=block, in_=block, func=RELU)
 
         def quantise_h(i, first, last):
-            c, g = divmod(i, PASSES)
+            if first == 0:
+                codes = hq_pool.tile([P, CHUNK], U32, align_bytes=64, name="h_codes")
+                scales = hq_pool.tile([P, CHUNK], U8, align_bytes=64, name="h_scales")
+                h_codes[i] = codes[:, :]
+                h_scales[i] = scales[:, :]
             edges = slice(first * P, last * P)
-            if g == 0 and first == 0:
-                h_codes[c] = hq_pool.tile([P, PASSES, CHUNK], U32, align_bytes=64, name="h_codes")
-                h_scales[c] = hq_pool.tile([P, PASSES, CHUNK], U8, align_bytes=64, name="h_scales")
             nc.vector.quantize_mx(
-                out=h_codes[c][:, g, edges].bitcast(FP8X4),
-                scales=h_scales[c][:, g, edges],
+                out=h_codes[i][:, edges].bitcast(FP8X4),
+                scales=h_scales[i][:, edges],
                 in_=h_grouped[i][:, edges, :].rearrange("r e t -> r (e t)"),
             )
+
+        joint = {}
+
+        def open_joint(i, c):
+            grouped = joint_pool.tile([P, 2 * CHUNK * PACK], BF16, align_bytes=64, name="joint_grouped")
+            codes = joint_pool.tile([P, 2 * CHUNK], U32, align_bytes=64, name="joint_codes")
+            scales = joint_pool.tile([P, 2 * CHUNK], U8, align_bytes=64, name="joint_scales")
+            h_grouped[i] = grouped[:, 0 : CHUNK * PACK].rearrange("r (e t) -> r e t", t=PACK)
+            h_codes[i] = codes[:, 0:CHUNK]
+            h_scales[i] = scales[:, 0:CHUNK]
+            x_grouped[c] = grouped[:, CHUNK * PACK :]
+            x_codes[c] = codes[:, CHUNK:]
+            x_scales[c] = scales[:, CHUNK:]
+            joint[i] = (grouped, codes, scales)
+
+        def quantise_joint(i):
+            grouped, codes, scales = joint[i]
+            nc.vector.quantize_mx(out=codes[:].bitcast(FP8X4), scales=scales[:], in_=grouped[:])
 
         y_sums = {}
         y_flipped = {}
@@ -323,8 +348,8 @@ def tile_edgenetwork_t_kernel(
                     out=y_sums[c, a][:],
                     lhsT=w2_codes[:, g, a * P : (a + 1) * P].bitcast(FP8X4),
                     lhsT_scale=w2_scales[:, g, a * P : (a + 1) * P],
-                    rhs=h_codes[c][:, g, :].bitcast(FP8X4),
-                    rhs_scale=h_scales[c][:, g, :],
+                    rhs=h_codes[i].bitcast(FP8X4),
+                    rhs_scale=h_scales[i],
                     start=(g == 0),
                     stop=(g == PASSES - 1),
                 )
@@ -351,8 +376,8 @@ def tile_edgenetwork_t_kernel(
                         out=bank[:, a, :],
                         lhsT=w2_codes[:, g, a * P : (a + 1) * P].bitcast(FP8X4),
                         lhsT_scale=w2_scales[:, g, a * P : (a + 1) * P],
-                        rhs=h_codes[c][:, g, edges].bitcast(FP8X4),
-                        rhs_scale=h_scales[c][:, g, edges],
+                        rhs=h_codes[c * PASSES + g][:, edges].bitcast(FP8X4),
+                        rhs_scale=h_scales[c * PASSES + g][:, edges],
                         start=(g == 0),
                         stop=(g == PASSES - 1),
                     )
@@ -388,6 +413,7 @@ def tile_edgenetwork_t_kernel(
         spread_edge(0, edge_bank(h_psum, "sums"))
         flip_w1(0, w1_bank(h_psum, "sums"), nc.vector.tensor_copy)
         quantise_w1(0)
+        open_x(0)
         flip_x(0, 0)
         flip_x(0, 1)
         first_terms_vector()
@@ -406,9 +432,12 @@ def tile_edgenetwork_t_kernel(
         last = N_CHUNKS - 1
         for i in range(SLOTS):
             c, g = divmod(i, PASSES)
-            if i == 0:
+            if i == 1:
+                open_x(1)
                 for two in range(2):
                     flip_x(1, two)
+            if g == 1 and c + 2 < N_CHUNKS:
+                open_joint(i, c + 2)
             if g == 0 and 1 <= c:
                 if 0 <= c - 2:
                     activate(c - 2, 1)
@@ -416,17 +445,17 @@ def tile_edgenetwork_t_kernel(
                     flip_x(c + 1, 1)
                 if 0 <= c - 3:
                     store_result(c - 3, 1, nc.scalar.copy)
-                second_matmul(i - 2)
-            if g == 1:
-                if 0 <= c - 1:
+                if 2 <= c:
                     second_matmul(i - 2)
+            if g == 1:
                 if c + 2 < N_CHUNKS:
                     flip_x(c + 2, 0)
                 if 0 <= c - 2:
                     store_result(c - 2, 0, nc.scalar.copy)
-                if 0 <= c - 1:
+                if 2 <= c:
+                    second_matmul(i - 2)
                     activate(c - 1, 0)
-            if i == 1:
+            if i == 2:
                 flip_w2()
             if i < SLOTS - 1:
                 add_term(i, 0)
@@ -435,15 +464,21 @@ def tile_edgenetwork_t_kernel(
                     quantise_w1(2)
                     quantise_w1(3)
                 rectify_vector(i, 0, 1)
+                if i == 3:
+                    quantise_w2()
+                    for k in range(PASSES):
+                        second_matmul(k)
+                    activate(0, 0)
+                rectify_scalar(i, 1, 2)
                 add_term(i, 2)
                 add_term(i, 3)
-                rectify_scalar(i, 1, BLOCKS)
-                if 1 <= i:
-                    quantise_h(i - 1, 0, BLOCKS)
                 if i == 1:
-                    quantise_w2()
-                if g == 0 and c + 1 < N_CHUNKS:
-                    quantise_x(c + 1, 0, BLOCKS)
+                    quantise_x(1, 0, BLOCKS)
+                rectify_scalar(i, 2, BLOCKS)
+                if i - 1 in joint:
+                    quantise_joint(i - 1)
+                elif 1 <= i:
+                    quantise_h(i - 1, 0, BLOCKS)
                 first_matmul(i + 1)
             if i < 2 * PASSES:
                 pair = 2 if i < PASSES else 4

@@ -63,7 +63,7 @@ def tile_edgenetwork_t_kernel(
         hq_pool = ctx.enter_context(tc.tile_pool(name="hidden_quantised", bufs=3))
         joint_pool = ctx.enter_context(tc.tile_pool(name="joint", bufs=3))
         yt_pool = ctx.enter_context(tc.tile_pool(name="result_flipped", bufs=3))
-        y_pool = ctx.enter_context(tc.tile_pool(name="result", bufs=4))
+        y_pool = ctx.enter_context(tc.tile_pool(name="result", bufs=6))
         flip_psum = ctx.enter_context(tc.psum_pool(name="flip", bufs=2))
         h_psum = ctx.enter_context(tc.psum_pool(name="hidden_sums", bufs=4))
         y_psum = ctx.enter_context(tc.psum_pool(name="result_sums", bufs=2))
@@ -129,8 +129,22 @@ def tile_edgenetwork_t_kernel(
 
         bias_flip = y_psum.tile([P, P], BF16, tag="y_sums")
         nc.tensor.transpose(bias_flip[:], bias_rows[:], identity_bf16[:])
+        bias_edge = keep.tile([P, M_TILES], F32)
+        nc.vector.tensor_copy(out=bias_edge[:], in_=bias_flip[:, 0:M_TILES])
         bias_cols = keep.tile([P, M_TILES + O_TILES], BF16)
         nc.vector.tensor_copy(out=bias_cols[:], in_=bias_flip[:, 0 : M_TILES + O_TILES])
+
+        b2_all = keep.tile([P, OUT], F32)
+        b2_spread = y_psum.tile([P, OUT], F32, tag="y_sums")
+        for a in range(O_TILES):
+            nc.tensor.matmul(
+                b2_spread[:, a * P : (a + 1) * P],
+                lhsT=identity_bf16[:, M_TILES + a : M_TILES + a + 1].to_broadcast([P, P]),
+                rhs=bias_rows[:],
+                start=True,
+                stop=True,
+            )
+        nc.scalar.copy(out=b2_all[:], in_=b2_spread[:])
 
         def spread_edge(c, bank):
             for k in range(2):
@@ -221,6 +235,7 @@ def tile_edgenetwork_t_kernel(
                 in_=x_grouped[c][:, first * P * PACK : last * P * PACK],
             )
 
+        w1_edge = keep.tile([P, M_TILES], F32)
         terms = {}
 
         def unquantised_term(c, n_chunks, g):
@@ -230,15 +245,14 @@ def tile_edgenetwork_t_kernel(
                 nc.gpsimd.tensor_scalar(
                     out=term[:, t, :],
                     in0=edge_all[:, c * CHUNK : (c + n_chunks) * CHUNK],
-                    scalar1=w1_rows[:, j, NODE : NODE + 1],
-                    scalar2=bias_cols[:, j : j + 1],
+                    scalar1=w1_edge[:, j : j + 1],
+                    scalar2=bias_edge[:, j : j + 1],
                     op0=MULT,
                     op1=ADD,
                 )
             for k in range(n_chunks):
                 terms[(c + k) * PASSES + g] = term[:, :, k * CHUNK : (k + 1) * CHUNK]
 
-        w1_edge = keep.tile([P, PACK], F32)
 
         def first_terms_vector():
             terms[0] = term_pool.tile([P, PACK, CHUNK], F32, name="term")
@@ -259,7 +273,7 @@ def tile_edgenetwork_t_kernel(
                     out=terms[1][:, t, :],
                     in_=edge_all[:, 0:CHUNK],
                     func=IDENTITY,
-                    scale=w1_edge[:, t : t + 1],
+                    scale=w1_edge[:, PACK + t : PACK + t + 1],
                     bias=bias_cols[:, PACK + t : PACK + t + 1],
                 )
 
@@ -364,45 +378,54 @@ def tile_edgenetwork_t_kernel(
                 bias=bias_cols[:, M_TILES + a : M_TILES + a + 1],
             )
 
-        def finish_half(c, two):
-            if two == 0:
-                y_flipped[c] = yt_pool.tile([P, O_TILES, CHUNK], F32, name="y_flipped")
-            half = CHUNK // 2
-            edges = slice(two * half, (two + 1) * half)
-            bank = h_psum.tile([P, O_TILES, half], F32, tag="sums", name="y_half")
-            for a in range(O_TILES):
+        def last_matmul(two):
+            bank = h_psum.tile([P, 2, OUT], F32, tag="sums", name="y_half")
+            for i in range(2):
+                edges = slice((2 * two + i) * P, (2 * two + i + 1) * P)
                 for g in range(PASSES):
+                    slot = (N_CHUNKS - 1) * PASSES + g
                     nc.tensor.matmul_mx(
-                        out=bank[:, a, :],
-                        lhsT=w2_codes[:, g, a * P : (a + 1) * P].bitcast(FP8X4),
-                        lhsT_scale=w2_scales[:, g, a * P : (a + 1) * P],
-                        rhs=h_codes[c * PASSES + g][:, edges].bitcast(FP8X4),
-                        rhs_scale=h_scales[c * PASSES + g][:, edges],
+                        out=bank[:, i, :],
+                        lhsT=h_codes[slot][:, edges].bitcast(FP8X4),
+                        lhsT_scale=h_scales[slot][:, edges],
+                        rhs=w2_codes[:, g, :].bitcast(FP8X4),
+                        rhs_scale=w2_scales[:, g, :],
                         start=(g == 0),
                         stop=(g == PASSES - 1),
                     )
-            for a in range(O_TILES):
-                nc.scalar.activation(
-                    out=y_flipped[c][:, a, edges],
-                    in_=bank[:, a, :],
-                    func=TANH,
-                    bias=bias_cols[:, M_TILES + a : M_TILES + a + 1],
-                )
+            return bank
 
         out_dram = out.rearrange("(b r) o -> r b o", r=P)
 
-        def store_result(c, two, copy):
-            y_flip = flip_psum.tile([P, 2, OUT], F32, tag="flip")
+        def result_bank(pool, tag):
+            return pool.tile([P, 2, OUT], F32, tag=tag, name="y_flip")
+
+        def flip_result(c, two, bank):
             for i in range(2):
                 edges = slice((2 * two + i) * P, (2 * two + i + 1) * P)
                 for a in range(O_TILES):
                     nc.tensor.transpose(
-                        y_flip[:, i, a * P : (a + 1) * P], y_flipped[c][:, a, edges], identity_f32[:]
+                        bank[:, i, a * P : (a + 1) * P], y_flipped[c][:, a, edges], identity_f32[:]
                     )
+
+        def store_result(c, two, bank, copy):
             y = y_pool.tile([P, 2, OUT], F32, name="y")
-            copy(out=y[:], in_=y_flip[:])
+            copy(out=y[:], in_=bank[:])
             first = c * BLOCKS + 2 * two
             nc.sync.dma_start(out=out_dram[:, first : first + 2, :], in_=y[:])
+
+        def finish_last(two, bank):
+            y = y_pool.tile([P, 2, OUT], F32, name="y")
+            for i in range(2):
+                nc.vector.tensor_tensor(out=y[:, i, :], in0=bank[:, i, :], in1=b2_all[:], op=ADD)
+                nc.scalar.activation(out=y[:, i, :], in_=y[:, i, :], func=TANH)
+            first = (N_CHUNKS - 1) * BLOCKS + 2 * two
+            nc.sync.dma_start(out=out_dram[:, first : first + 2, :], in_=y[:])
+
+        def finish_result(c, two):
+            bank = result_bank(flip_psum, "flip")
+            flip_result(c, two, bank)
+            store_result(c, two, bank, nc.scalar.copy)
 
         def w1_bank(pool, tag):
             return pool.tile([P, 2, 2, P], F32, tag=tag, name="w1_flip")
@@ -423,7 +446,7 @@ def tile_edgenetwork_t_kernel(
         quantise_x(0, 2, BLOCKS)
         flip_w1(2, w1_bank(y_psum, "y_sums"), nc.scalar.copy)
         flip_w1(3, w1_bank(y_psum, "y_sums"), nc.scalar.copy)
-        nc.vector.tensor_copy(out=w1_edge[:], in_=w1_rows[:, PACK:M_TILES, NODE])
+        nc.vector.tensor_copy(out=w1_edge[:], in_=w1_rows[:, :, NODE])
         first_terms_scalar()
         for g in range(PASSES):
             unquantised_term(1, 1, g)
@@ -444,14 +467,14 @@ def tile_edgenetwork_t_kernel(
                 if c + 1 < N_CHUNKS:
                     flip_x(c + 1, 1)
                 if 0 <= c - 3:
-                    store_result(c - 3, 1, nc.scalar.copy)
+                    finish_result(c - 3, 1)
                 if 2 <= c:
                     second_matmul(i - 2)
             if g == 1:
                 if c + 2 < N_CHUNKS:
                     flip_x(c + 2, 0)
                 if 0 <= c - 2:
-                    store_result(c - 2, 0, nc.scalar.copy)
+                    finish_result(c - 2, 0)
                 if 2 <= c:
                     second_matmul(i - 2)
                     activate(c - 1, 0)
@@ -463,13 +486,15 @@ def tile_edgenetwork_t_kernel(
                 if i == 0:
                     quantise_w1(2)
                     quantise_w1(3)
-                rectify_vector(i, 0, 1)
+                scalar_first = 0 if 1 <= i < 2 * PASSES else 1
+                if scalar_first == 1:
+                    rectify_vector(i, 0, 1)
                 if i == 3:
                     quantise_w2()
                     for k in range(PASSES):
                         second_matmul(k)
                     activate(0, 0)
-                rectify_scalar(i, 1, 2)
+                rectify_scalar(i, scalar_first, 2)
                 add_term(i, 2)
                 add_term(i, 3)
                 if i == 1:
@@ -488,7 +513,8 @@ def tile_edgenetwork_t_kernel(
 
         i = SLOTS - 1
         activate(last - 1, 1)
-        store_result(last - 2, 1, nc.scalar.copy)
+        finish_result(last - 2, 1)
+        finish_result(last - 1, 0)
         add_term(i, 0)
         add_term(i, 1)
         rectify_vector(i, 0, 1)
@@ -496,12 +522,11 @@ def tile_edgenetwork_t_kernel(
         rectify_vector(i, 1, 2)
         quantise_h(i - 1, 0, BLOCKS)
         add_term(i, 3)
-        quantise_h(i, 0, 2)
         rectify_vector(i, 2, BLOCKS)
-        finish_half(last, 0)
+        quantise_h(i, 0, 2)
+        finish_result(last - 1, 1)
+        halves = [last_matmul(0)]
         quantise_h(i, 2, BLOCKS)
-        store_result(last - 1, 0, nc.vector.tensor_copy)
-        finish_half(last, 1)
-        store_result(last - 1, 1, nc.vector.tensor_copy)
-        store_result(last, 0, nc.scalar.copy)
-        store_result(last, 1, nc.vector.tensor_copy)
+        halves.append(last_matmul(1))
+        for two in range(2):
+            finish_last(two, halves[two])

from contextlib import ExitStack

import concourse.mybir as mybir
from concourse.masks import make_identity

F32 = mybir.dt.float32
BF16 = mybir.dt.bfloat16
U32 = mybir.dt.uint32
U8 = mybir.dt.uint8
FP8X4 = mybir.dt.float8_e4m3fn_x4
ADD = mybir.AluOpType.add
MULT = mybir.AluOpType.mult
RELU = mybir.ActivationFunctionType.Relu
TANH = mybir.ActivationFunctionType.Tanh
IDENTITY = mybir.ActivationFunctionType.Identity

P = 128
PACK = 4
EDGES, FEAT, HIDDEN, MID, OUT = 4096, 64, 192, 1024, 256
NODE = 2 * (FEAT + HIDDEN)
FLOPS = 2 * EDGES * ((NODE + 1) * MID + MID * OUT)

CHUNK = 512
BLOCKS = CHUNK // P
N_CHUNKS = EDGES // CHUNK
M_TILES = MID // P
PASSES = M_TILES // PACK
O_TILES = OUT // P
SLOTS = N_CHUNKS * PASSES
W1_PITCH = NODE + 16


def transpose_words(nc, bank, rows, identity):
    for b in range(2):
        for u in range(2):
            nc.tensor.transpose(bank[:, b, u, :], rows[:, b, u * P : (u + 1) * P], identity)


def grouped_words(grouped):
    return grouped.bitcast(F32).rearrange("q (b r u) -> q b r u", r=P, u=2)


def tile_edgenetwork_t_kernel(
    tc,
    dst_node_feat,
    dst_node_hidden,
    src_node_feat,
    src_node_hidden,
    edge_feat,
    W1,
    b1,
    W2,
    b2,
    out,
):
    nc = tc.nc
    with ExitStack() as ctx:
        keep = ctx.enter_context(tc.tile_pool(name="keep", bufs=1))
        x_pool = ctx.enter_context(tc.tile_pool(name="x_rows", bufs=N_CHUNKS))
        xq_pool = ctx.enter_context(tc.tile_pool(name="x_quantised", bufs=2))
        term_pool = ctx.enter_context(tc.tile_pool(name="term", bufs=4))
        h_pool = ctx.enter_context(tc.tile_pool(name="hidden", bufs=4))
        hq_pool = ctx.enter_context(tc.tile_pool(name="hidden_quantised", bufs=3))
        joint_pool = ctx.enter_context(tc.tile_pool(name="joint", bufs=3))
        yt_pool = ctx.enter_context(tc.tile_pool(name="result_flipped", bufs=3))
        y_pool = ctx.enter_context(tc.tile_pool(name="result", bufs=6))
        flip_psum = ctx.enter_context(tc.psum_pool(name="flip", bufs=2))
        h_psum = ctx.enter_context(tc.psum_pool(name="hidden_sums", bufs=4))
        y_psum = ctx.enter_context(tc.psum_pool(name="result_sums", bufs=2))
        ctx.enter_context(tc.manual_schedule())

        warm = keep.tile([P, 1], F32)
        nc.vector.memset(warm[:], 0.0)
        nc.scalar.activation(out=warm[:], in_=warm[:], func=TANH)

        w1_rows = keep.tile([P, M_TILES, W1_PITCH], BF16)
        w1_dram = W1.rearrange("(j r) k -> r j k", r=P)
        x_parts = (
            (dst_node_feat, 0, FEAT),
            (dst_node_hidden, FEAT, HIDDEN),
            (src_node_feat, FEAT + HIDDEN, FEAT),
            (src_node_hidden, 2 * FEAT + HIDDEN, HIDDEN),
        )
        x_rows = []

        def load_w1(two):
            tiles = slice(2 * two, 2 * two + 2)
            nc.sync.dma_start(out=w1_rows[:, tiles, 0 : NODE + 1], in_=w1_dram[:, tiles, :])

        def load_x(c):
            rows = x_pool.tile([P, BLOCKS, NODE], BF16, name="x_rows")
            for part, first, width in x_parts:
                nc.sync.dma_start(
                    out=rows[:, :, first : first + width],
                    in_=part.rearrange("(b r) f -> r b f", r=P)[:, c * BLOCKS : (c + 1) * BLOCKS, :],
                )
            x_rows.append(rows)

        bias_rows = keep.tile([P, P], BF16)
        nc.vector.memset(bias_rows[:], 0.0)
        edge_rows = keep.tile([P, CHUNK], BF16)
        nc.vector.memset(edge_rows[:], 0.0)
        edge_all = keep.tile([P, EDGES], BF16)
        w2_rows = keep.tile([P, O_TILES, MID], BF16)

        nc.sync.dma_start(out=bias_rows[0:M_TILES, :], in_=b1.rearrange("(j r) -> j r", r=P))
        nc.sync.dma_start(
            out=bias_rows[M_TILES : M_TILES + O_TILES, :], in_=b2.rearrange("(a r) -> a r", r=P)
        )
        nc.sync.dma_start(out=edge_rows[0:N_CHUNKS, :], in_=edge_feat.rearrange("(c e) -> c e", e=CHUNK))
        load_w1(0)
        load_x(0)
        load_w1(1)
        load_w1(2)
        load_w1(3)
        load_x(1)
        load_x(2)
        nc.sync.dma_start(out=w2_rows[:], in_=W2.rearrange("(a r) m -> r a m", r=P))
        nc.sync.dma_start(
            out=edge_all[:, 2 * CHUNK :], in_=edge_feat[2 * CHUNK : EDGES].partition_broadcast(P)
        )
        for c in range(3, N_CHUNKS):
            load_x(c)

        identity_bf16 = keep.tile([P, P], BF16)
        make_identity(nc, identity_bf16[:])
        identity_f32 = keep.tile([P, P], F32)
        make_identity(nc, identity_f32[:])

        bias_flip = y_psum.tile([P, P], BF16, tag="y_sums")
        nc.tensor.transpose(bias_flip[:], bias_rows[:], identity_bf16[:])
        bias_edge = keep.tile([P, M_TILES], F32)
        nc.vector.tensor_copy(out=bias_edge[:], in_=bias_flip[:, 0:M_TILES])
        bias_cols = keep.tile([P, M_TILES + O_TILES], BF16)
        nc.vector.tensor_copy(out=bias_cols[:], in_=bias_flip[:, 0 : M_TILES + O_TILES])

        b2_all = keep.tile([P, OUT], F32)
        b2_spread = y_psum.tile([P, OUT], F32, tag="y_sums")
        for a in range(O_TILES):
            nc.tensor.matmul(
                b2_spread[:, a * P : (a + 1) * P],
                lhsT=identity_bf16[:, M_TILES + a : M_TILES + a + 1].to_broadcast([P, P]),
                rhs=bias_rows[:],
                start=True,
                stop=True,
            )
        nc.scalar.copy(out=b2_all[:], in_=b2_spread[:])

        def spread_edge(c, bank):
            for k in range(2):
                nc.tensor.matmul(
                    bank[:, k, :],
                    lhsT=identity_bf16[:, c + k : c + k + 1].to_broadcast([P, P]),
                    rhs=edge_rows[:],
                    start=True,
                    stop=True,
                )
            nc.scalar.copy(
                out=edge_all[:, c * CHUNK : (c + 2) * CHUNK], in_=bank[:].rearrange("p k e -> p (k e)")
            )

        w1_words = w1_rows[:].bitcast(F32)
        w1_grouped = keep.tile([P, MID * PACK], BF16, align_bytes=64)
        w1_codes = keep.tile([P, MID], U32, align_bytes=64)
        w1_scales = keep.tile([P, MID], U8, align_bytes=64)

        def flip_w1(two, bank, copy):
            tiles = slice(2 * two, 2 * two + 2)
            transpose_words(nc, bank, w1_words[:, tiles, :], identity_f32[:])
            copy(
                out=grouped_words(w1_grouped[:])[:, tiles, :, :],
                in_=bank[:].rearrange("q b u r -> q b r u"),
            )

        def quantise_w1(two):
            units = slice(two * 2 * P, (two + 1) * 2 * P)
            nc.vector.quantize_mx(
                out=w1_codes[:, units].bitcast(FP8X4),
                scales=w1_scales[:, units],
                in_=w1_grouped[:, two * 2 * P * PACK : (two + 1) * 2 * P * PACK],
            )

        w2_grouped = keep.tile([P, PASSES, OUT, PACK], BF16, align_bytes=64)
        w2_codes = keep.tile([P, PASSES, OUT], U32, align_bytes=64)
        w2_scales = keep.tile([P, PASSES, OUT], U8, align_bytes=64)

        def flip_w2():
            for g in range(PASSES):
                w2_flip = y_psum.tile([P, PACK, OUT], BF16, tag="y_sums")
                for t in range(PACK):
                    for a in range(O_TILES):
                        first = (g * PACK + t) * P
                        nc.tensor.transpose(
                            w2_flip[:, t, a * P : (a + 1) * P],
                            w2_rows[:, a, first : first + P],
                            identity_bf16[:],
                        )
                nc.scalar.copy(
                    out=w2_grouped[:, g, :, :], in_=w2_flip[:].rearrange("r t o -> r o t")
                )

        def quantise_w2():
            nc.vector.quantize_mx(
                out=w2_codes[:].rearrange("r g o -> r (g o)").bitcast(FP8X4),
                scales=w2_scales[:].rearrange("r g o -> r (g o)"),
                in_=w2_grouped[:].rearrange("r g o t -> r (g o t)"),
            )

        x_grouped = {}
        x_codes = {}
        x_scales = {}

        def flip_x(c, two):
            blocks = slice(2 * two, 2 * two + 2)
            x_flip = flip_psum.tile([P, 2, 2, P], F32, tag="flip")
            transpose_words(nc, x_flip, x_rows[c][:].bitcast(F32)[:, blocks, :], identity_f32[:])
            nc.scalar.copy(
                out=grouped_words(x_grouped[c])[:, blocks, :, :],
                in_=x_flip[:].rearrange("q b u r -> q b r u"),
            )

        def open_x(c):
            grouped = xq_pool.tile([P, CHUNK * PACK], BF16, align_bytes=64, name="x_grouped")
            codes = xq_pool.tile([P, CHUNK], U32, align_bytes=64, name="x_codes")
            scales = xq_pool.tile([P, CHUNK], U8, align_bytes=64, name="x_scales")
            x_grouped[c] = grouped[:, :]
            x_codes[c] = codes[:, :]
            x_scales[c] = scales[:, :]

        def quantise_x(c, first, last):
            edges = slice(first * P, last * P)
            nc.vector.quantize_mx(
                out=x_codes[c][:, edges].bitcast(FP8X4),
                scales=x_scales[c][:, edges],
                in_=x_grouped[c][:, first * P * PACK : last * P * PACK],
            )

        w1_edge = keep.tile([P, M_TILES], F32)
        terms = {}

        def unquantised_term(c, n_chunks, g):
            term = term_pool.tile([P, PACK, n_chunks * CHUNK], F32, name="term")
            for t in range(PACK):
                j = g * PACK + t
                nc.gpsimd.tensor_scalar(
                    out=term[:, t, :],
                    in0=edge_all[:, c * CHUNK : (c + n_chunks) * CHUNK],
                    scalar1=w1_edge[:, j : j + 1],
                    scalar2=bias_edge[:, j : j + 1],
                    op0=MULT,
                    op1=ADD,
                )
            for k in range(n_chunks):
                terms[(c + k) * PASSES + g] = term[:, :, k * CHUNK : (k + 1) * CHUNK]


        def first_terms_vector():
            terms[0] = term_pool.tile([P, PACK, CHUNK], F32, name="term")
            for t in range(PACK):
                nc.vector.tensor_scalar(
                    out=terms[0][:, t, :],
                    in0=edge_all[:, 0:CHUNK],
                    scalar1=w1_rows[:, t, NODE : NODE + 1],
                    scalar2=bias_cols[:, t : t + 1],
                    op0=MULT,
                    op1=ADD,
                )

        def first_terms_scalar():
            terms[1] = term_pool.tile([P, PACK, CHUNK], F32, name="term")
            for t in range(PACK):
                nc.scalar.activation(
                    out=terms[1][:, t, :],
                    in_=edge_all[:, 0:CHUNK],
                    func=IDENTITY,
                    scale=w1_edge[:, PACK + t : PACK + t + 1],
                    bias=bias_cols[:, PACK + t : PACK + t + 1],
                )

        sums = {}
        h_grouped = {}
        h_codes = {}
        h_scales = {}

        def first_matmul(i):
            c, g = divmod(i, PASSES)
            for b in range(BLOCKS):
                edges = slice(b * P, (b + 1) * P)
                sums[i, b] = h_psum.tile([P, PACK, P], F32, tag="sums", name="sums")
                for t in range(PACK):
                    j = g * PACK + t
                    nc.tensor.matmul_mx(
                        out=sums[i, b][:, t, :],
                        lhsT=w1_codes[:, j * P : (j + 1) * P].bitcast(FP8X4),
                        lhsT_scale=w1_scales[:, j * P : (j + 1) * P],
                        rhs=x_codes[c][:, edges].bitcast(FP8X4),
                        rhs_scale=x_scales[c][:, edges],
                        start=True,
                        stop=True,
                    )

        def add_term(i, b):
            if b == 0 and i not in h_grouped:
                h_tile = h_pool.tile([P, CHUNK, PACK], BF16, align_bytes=64, name="h_grouped")
                h_grouped[i] = h_tile[:, :, :]
            edges = slice(b * P, (b + 1) * P)
            nc.vector.tensor_tensor(
                out=h_grouped[i][:, edges, :].rearrange("r (n i) t -> r n t i", i=PACK),
                in0=sums[i, b][:].rearrange("r t (n i) -> r n t i", i=PACK),
                in1=terms[i][:, :, edges].rearrange("r t (n i) -> r n t i", i=PACK),
                op=ADD,
            )

        def rectify_vector(i, first, last):
            block = h_grouped[i][:, first * P : last * P, :]
            nc.vector.tensor_scalar_max(block, block, 0.0)

        def rectify_scalar(i, first, last):
            block = h_grouped[i][:, first * P : last * P, :]
            nc.scalar.activation(out=block, in_=block, func=RELU)

        def quantise_h(i, first, last):
            if first == 0:
                codes = hq_pool.tile([P, CHUNK], U32, align_bytes=64, name="h_codes")
                scales = hq_pool.tile([P, CHUNK], U8, align_bytes=64, name="h_scales")
                h_codes[i] = codes[:, :]
                h_scales[i] = scales[:, :]
            edges = slice(first * P, last * P)
            nc.vector.quantize_mx(
                out=h_codes[i][:, edges].bitcast(FP8X4),
                scales=h_scales[i][:, edges],
                in_=h_grouped[i][:, edges, :].rearrange("r e t -> r (e t)"),
            )

        joint = {}

        def open_joint(i, c):
            grouped = joint_pool.tile([P, 2 * CHUNK * PACK], BF16, align_bytes=64, name="joint_grouped")
            codes = joint_pool.tile([P, 2 * CHUNK], U32, align_bytes=64, name="joint_codes")
            scales = joint_pool.tile([P, 2 * CHUNK], U8, align_bytes=64, name="joint_scales")
            h_grouped[i] = grouped[:, 0 : CHUNK * PACK].rearrange("r (e t) -> r e t", t=PACK)
            h_codes[i] = codes[:, 0:CHUNK]
            h_scales[i] = scales[:, 0:CHUNK]
            x_grouped[c] = grouped[:, CHUNK * PACK :]
            x_codes[c] = codes[:, CHUNK:]
            x_scales[c] = scales[:, CHUNK:]
            joint[i] = (grouped, codes, scales)

        def quantise_joint(i):
            grouped, codes, scales = joint[i]
            nc.vector.quantize_mx(out=codes[:].bitcast(FP8X4), scales=scales[:], in_=grouped[:])

        y_sums = {}
        y_flipped = {}

        def second_matmul(i):
            c, g = divmod(i, PASSES)
            for a in range(O_TILES):
                if g == 0:
                    y_sums[c, a] = y_psum.tile([P, CHUNK], F32, tag="y_sums", name="y_sums")
                nc.tensor.matmul_mx(
                    out=y_sums[c, a][:],
                    lhsT=w2_codes[:, g, a * P : (a + 1) * P].bitcast(FP8X4),
                    lhsT_scale=w2_scales[:, g, a * P : (a + 1) * P],
                    rhs=h_codes[i].bitcast(FP8X4),
                    rhs_scale=h_scales[i],
                    start=(g == 0),
                    stop=(g == PASSES - 1),
                )

        def activate(c, a):
            if a == 0:
                y_flipped[c] = yt_pool.tile([P, O_TILES, CHUNK], F32, name="y_flipped")
            nc.scalar.activation(
                out=y_flipped[c][:, a, :],
                in_=y_sums[c, a][:],
                func=TANH,
                bias=bias_cols[:, M_TILES + a : M_TILES + a + 1],
            )

        def last_matmul(two):
            bank = h_psum.tile([P, 2, OUT], F32, tag="sums", name="y_half")
            for i in range(2):
                edges = slice((2 * two + i) * P, (2 * two + i + 1) * P)
                for g in range(PASSES):
                    slot = (N_CHUNKS - 1) * PASSES + g
                    nc.tensor.matmul_mx(
                        out=bank[:, i, :],
                        lhsT=h_codes[slot][:, edges].bitcast(FP8X4),
                        lhsT_scale=h_scales[slot][:, edges],
                        rhs=w2_codes[:, g, :].bitcast(FP8X4),
                        rhs_scale=w2_scales[:, g, :],
                        start=(g == 0),
                        stop=(g == PASSES - 1),
                    )
            return bank

        out_dram = out.rearrange("(b r) o -> r b o", r=P)

        def result_bank(pool, tag):
            return pool.tile([P, 2, OUT], F32, tag=tag, name="y_flip")

        def flip_result(c, two, bank):
            for i in range(2):
                edges = slice((2 * two + i) * P, (2 * two + i + 1) * P)
                for a in range(O_TILES):
                    nc.tensor.transpose(
                        bank[:, i, a * P : (a + 1) * P], y_flipped[c][:, a, edges], identity_f32[:]
                    )

        def store_result(c, two, bank, copy):
            y = y_pool.tile([P, 2, OUT], F32, name="y")
            copy(out=y[:], in_=bank[:])
            first = c * BLOCKS + 2 * two
            nc.sync.dma_start(out=out_dram[:, first : first + 2, :], in_=y[:])

        def finish_last(two, bank):
            y = y_pool.tile([P, 2, OUT], F32, name="y")
            for i in range(2):
                nc.vector.tensor_tensor(out=y[:, i, :], in0=bank[:, i, :], in1=b2_all[:], op=ADD)
                nc.scalar.activation(out=y[:, i, :], in_=y[:, i, :], func=TANH)
            first = (N_CHUNKS - 1) * BLOCKS + 2 * two
            nc.sync.dma_start(out=out_dram[:, first : first + 2, :], in_=y[:])

        def finish_result(c, two):
            bank = result_bank(flip_psum, "flip")
            flip_result(c, two, bank)
            store_result(c, two, bank, nc.scalar.copy)

        def w1_bank(pool, tag):
            return pool.tile([P, 2, 2, P], F32, tag=tag, name="w1_flip")

        def edge_bank(pool, tag):
            return pool.tile([P, 2, CHUNK], BF16, tag=tag, name="edge_spread")

        spread_edge(0, edge_bank(h_psum, "sums"))
        flip_w1(0, w1_bank(h_psum, "sums"), nc.vector.tensor_copy)
        quantise_w1(0)
        open_x(0)
        flip_x(0, 0)
        flip_x(0, 1)
        first_terms_vector()
        flip_w1(1, w1_bank(h_psum, "sums"), nc.vector.tensor_copy)
        quantise_x(0, 0, 2)
        quantise_w1(1)
        quantise_x(0, 2, BLOCKS)
        flip_w1(2, w1_bank(y_psum, "y_sums"), nc.scalar.copy)
        flip_w1(3, w1_bank(y_psum, "y_sums"), nc.scalar.copy)
        nc.vector.tensor_copy(out=w1_edge[:], in_=w1_rows[:, :, NODE])
        first_terms_scalar()
        for g in range(PASSES):
            unquantised_term(1, 1, g)
        first_matmul(0)

        last = N_CHUNKS - 1
        for i in range(SLOTS):
            c, g = divmod(i, PASSES)
            if i == 1:
                open_x(1)
                for two in range(2):
                    flip_x(1, two)
            if g == 1 and c + 2 < N_CHUNKS:
                open_joint(i, c + 2)
            if g == 0 and 1 <= c:
                if 0 <= c - 2:
                    activate(c - 2, 1)
                if c + 1 < N_CHUNKS:
                    flip_x(c + 1, 1)
                if 0 <= c - 3:
                    finish_result(c - 3, 1)
                if 2 <= c:
                    second_matmul(i - 2)
            if g == 1:
                if c + 2 < N_CHUNKS:
                    flip_x(c + 2, 0)
                if 0 <= c - 2:
                    finish_result(c - 2, 0)
                if 2 <= c:
                    second_matmul(i - 2)
                    activate(c - 1, 0)
            if i == 2:
                flip_w2()
            if i < SLOTS - 1:
                add_term(i, 0)
                add_term(i, 1)
                if i == 0:
                    quantise_w1(2)
                    quantise_w1(3)
                scalar_first = 0 if 1 <= i < 2 * PASSES else 1
                if scalar_first == 1:
                    rectify_vector(i, 0, 1)
                if i == 3:
                    quantise_w2()
                    for k in range(PASSES):
                        second_matmul(k)
                    activate(0, 0)
                rectify_scalar(i, scalar_first, 2)
                add_term(i, 2)
                add_term(i, 3)
                if i == 1:
                    quantise_x(1, 0, BLOCKS)
                rectify_scalar(i, 2, BLOCKS)
                if i - 1 in joint:
                    quantise_joint(i - 1)
                elif 1 <= i:
                    quantise_h(i - 1, 0, BLOCKS)
                first_matmul(i + 1)
            if i < 2 * PASSES:
                pair = 2 if i < PASSES else 4
                unquantised_term(pair, 2, g)
            elif 3 * PASSES <= i < 4 * PASSES:
                unquantised_term(6, 2, g)

        i = SLOTS - 1
        activate(last - 1, 1)
        finish_result(last - 2, 1)
        finish_result(last - 1, 0)
        add_term(i, 0)
        add_term(i, 1)
        rectify_vector(i, 0, 1)
        add_term(i, 2)
        rectify_vector(i, 1, 2)
        quantise_h(i - 1, 0, BLOCKS)
        add_term(i, 3)
        rectify_vector(i, 2, BLOCKS)
        quantise_h(i, 0, 2)
        finish_result(last - 1, 1)
        halves = [last_matmul(0)]
        quantise_h(i, 2, BLOCKS)
        halves.append(last_matmul(1))
        for two in range(2):
            finish_last(two, halves[two])
